import numpy as np
import ml_dtypes


def mxq(x, axis, fmt="e4m3"):
    dtype, down = {"e4m3": (ml_dtypes.float8_e4m3fn, 7), "e5m2": (ml_dtypes.float8_e5m2, 14)}[fmt]
    v = np.moveaxis(np.asarray(x, np.float32).astype(ml_dtypes.bfloat16).astype(np.float64), axis, -1)
    blocks = v.reshape(v.shape[:-1] + (-1, 32))
    amax = np.abs(blocks).max(-1, keepdims=True)
    byte = np.maximum(np.where(amax > 0, np.frexp(amax)[1] - 1 + 127, 0) - down, 1)
    scale = np.exp2(byte - 127.0)
    codes = (blocks / scale).astype(np.float32).astype(dtype).astype(np.float64)
    return np.moveaxis((codes * scale).reshape(v.shape), -1, axis)


WIDE = False


def mx_kscale(k):
    if not WIDE:
        return np.ones(k)
    levels = np.array([10, -10, 5, -5, 0])
    if k % 512:
        return np.exp2(np.random.permutation(np.resize(levels, k // 32))).repeat(32)
    a = np.empty((k // 512, 16))
    for p in range(k // 512):
        a[p, :8] = np.random.permutation(np.resize(levels, 8))
        for g in range(8):
            far = levels[np.abs(levels - a[p, g]) >= 10]
            a[p, g + 8] = far[np.random.randint(len(far))]
    return np.exp2(a.ravel()).repeat(32)


BF16 = ml_dtypes.bfloat16


def bf(x):
    return np.asarray(x, np.float32).astype(BF16)


def f64(x):
    return np.asarray(x).astype(np.float64)


B, K, N = 2048, 1024, 1024
EPS = 1e-7
MIN_NORM = 1e-15
MAX_TANH_ARG = 15.0


def _cosh(v):
    return 0.5 * (np.exp(v) + np.exp(-v))


def _sinh(v):
    return 0.5 * (np.exp(v) - np.exp(-v))


def _arccosh(v):
    return np.log(v + np.sqrt(v * v - 1.0))


def _norm(v):
    return np.sqrt(np.sum(v * v, axis=-1, keepdims=True))


def _mink_dot(u, v):
    return -u[..., :1] * v[..., :1] + np.sum(u[..., 1:] * v[..., 1:], axis=-1, keepdims=True)


def _proj(x):
    sp = x[..., 1:]
    t = np.sqrt(1.0 + np.sum(sp * sp, axis=-1, keepdims=True))
    return np.concatenate([t, sp], axis=-1)


def _proj_tan(u, x):
    ux = np.sum(x[..., 1:] * u[..., 1:], axis=-1, keepdims=True)
    t = ux / np.maximum(x[..., :1], MIN_NORM)
    return np.concatenate([t, u[..., 1:]], axis=-1)


def logmap_0(x):
    sp = x[..., 1:]
    n = np.maximum(_norm(sp), MIN_NORM)
    theta = np.maximum(x[..., :1], 1.0 + EPS)
    out_sp = _arccosh(theta) * sp / n
    return np.concatenate([np.zeros_like(theta), out_sp], axis=-1)


def expmap_0(u, backproject=True):
    sp = u[..., 1:]
    n = np.maximum(_norm(sp), MIN_NORM)
    theta = np.minimum(n, MAX_TANH_ARG)
    t = _cosh(theta)
    out_sp = _sinh(theta) * sp / n
    res = np.concatenate([t, out_sp], axis=-1)
    return _proj(res) if backproject else res


def ptransp_0(u, x):
    x0 = x[..., :1]
    y = x[..., 1:]
    y_norm = np.maximum(_norm(y), MIN_NORM)
    y_hat = y / y_norm
    v_time = -y_norm
    v_space = (1.0 - x0) * y_hat
    alpha = np.sum(y_hat * u[..., 1:], axis=-1, keepdims=True)
    res_time = np.zeros_like(x0) - alpha * v_time
    res_space = u[..., 1:] - alpha * v_space
    res = np.concatenate([res_time, res_space], axis=-1)
    return _proj_tan(res, x)


def expmap(u, x, backproject=True):
    unorm = np.sqrt(np.maximum(_mink_dot(u, u), MIN_NORM))
    theta = np.minimum(np.maximum(unorm, MIN_NORM), MAX_TANH_ARG)
    res = _cosh(theta) * x + _sinh(theta) * u / theta
    return _proj(res) if backproject else res


def setup_inputs():
    s = mx_kscale(K)
    c = np.sqrt(np.mean(s * s))
    sp = (np.random.standard_normal((B, K)) + 1.0) * (4.0 / np.sqrt(2.0 * K)) * (0.5 + np.random.random((B, 1)))
    sp = sp * s[None, :] / c
    t = np.sqrt(1.0 + np.sum(sp * sp, axis=-1, keepdims=True))
    w0 = np.random.standard_normal((N, K)) * (0.8 / np.sqrt(N))
    p = w0.sum(axis=1)
    b = 0.5 * np.random.standard_normal((1, N)) / np.sqrt(N) + 0.5 * p[None, :] / np.sqrt(np.sum(p * p))
    return {"x": bf(np.concatenate([t, sp], axis=-1)), "weight": bf(w0 / s[None, :] * c), "bias": bf(b)}


def reference(x, weight, bias):
    x, weight, bias = f64(x), f64(weight), f64(bias)
    u = logmap_0(x)
    h_sp = mxq(u[..., 1:], 1, "e4m3") @ mxq(weight, 1, "e4m3").T
    h = np.concatenate([np.zeros_like(h_sp[..., :1]), h_sp], axis=-1)
    m = expmap_0(h, backproject=True)
    b = np.concatenate([np.zeros_like(bias[..., :1]), bias], axis=-1)
    b = np.broadcast_to(b, m.shape)
    pt_b = ptransp_0(b, m)
    return expmap(pt_b, m, backproject=True)

@@ -1,0 +1,372 @@
+from contextlib import ExitStack
+
+import concourse.mybir as mybir
+from concourse.masks import make_identity
+
+FP8X4 = mybir.dt.float8_e4m3fn_x4
+BF16 = mybir.dt.bfloat16
+F32 = mybir.dt.float32
+U32 = mybir.dt.uint32
+U8 = mybir.dt.uint8
+ALU = mybir.AluOpType
+ACT = mybir.ActivationFunctionType
+
+P = 128
+ROWS = 2048
+K = 1024
+N = 1024
+TILES = ROWS // P
+K_PASS = 512
+PASSES = K // K_PASS
+BANK = 512
+BANKS = N // BANK
+W_CHUNK = 256
+W_CHUNKS = N // W_CHUNK
+X_SLOT = 1040
+AHEAD_NORM = 4
+AHEAD_LOG_MAP = 3
+AHEAD_REGROUP = 2
+AHEAD_MATMUL = 1
+
+FLOPS = 2 * ROWS * K * N
+
+
+def tile_hyperboliclinearhyperboloid_kernel(tc, x, weight, bias, out):
+    nc = tc.nc
+    with ExitStack() as stack:
+        keep = stack.enter_context(tc.tile_pool(name="keep", bufs=1))
+        wstage = stack.enter_context(tc.tile_pool(name="wstage", bufs=4))
+        upool = stack.enter_context(tc.tile_pool(name="upool", bufs=4))
+        opool = stack.enter_context(tc.tile_pool(name="opool", bufs=4))
+        junk = stack.enter_context(tc.tile_pool(name="junk", bufs=3))
+        small = stack.enter_context(tc.tile_pool(name="small", bufs=8))
+        psum_t = stack.enter_context(tc.psum_pool(name="psum_t", bufs=1))
+        psum_h = stack.enter_context(tc.psum_pool(name="psum_h", bufs=7))
+        stack.enter_context(tc.manual_schedule())
+
+        x_rows = x.rearrange("(p t) c -> p t c", t=TILES)
+        out_rows = out.rearrange("(p t) c -> p t c", t=TILES)
+        w_rows = weight.rearrange("(c b p) k -> p c b k", b=W_CHUNK // P, p=P)
+
+        x_head = keep.tile([P, TILES, 16], BF16)
+        bias_bc = keep.tile([P, N], BF16)
+        x_sb = keep.tile([P, TILES, X_SLOT], BF16)
+        w_sb = keep.tile([P, W_CHUNKS, W_CHUNK // P, K], BF16)
+
+        def load_x(t0, t1):
+            nc.sync.dma_start(out=x_sb[:, t0:t1, 1 : K + 2], in_=x_rows[:, t0:t1, :])
+
+        def load_w(c):
+            nc.sync.dma_start(out=w_sb[:, c, :, :], in_=w_rows[:, c, :, :])
+
+        nc.sync.dma_start(out=x_head[:], in_=x_rows[:, :, 0:16])
+        load_x(0, 2)
+        nc.sync.dma_start(out=bias_bc[:], in_=bias.rearrange("a b -> (a b)").partition_broadcast(P))
+        load_w(0)
+        load_w(1)
+        load_x(2, 4)
+        load_w(2)
+        load_w(3)
+        load_x(4, 6)
+        load_x(6, 8)
+        load_x(8, 12)
+        load_x(12, 16)
+
+        ident_f = keep.tile([P, P], F32)
+        make_identity(nc, ident_f[:])
+        half = keep.tile([P, 1], F32)
+        nc.vector.memset(half[:], 0.5)
+        minus_half = keep.tile([P, 1], F32)
+        nc.vector.memset(minus_half[:], -0.5)
+        warm = keep.tile([P, 1], F32)
+        nc.scalar.activation(out=warm[:], in_=half[:], func=ACT.Sqrt)
+
+        theta0 = keep.tile([P, TILES], F32)
+        nc.vector.tensor_scalar(out=theta0[:], in0=x_head[:, :, 0], scalar1=1.0 + 1e-7, scalar2=None, op0=ALU.max)
+        theta0_m1 = keep.tile([P, TILES], F32)
+        nc.vector.tensor_scalar(out=theta0_m1[:], in0=theta0[:], scalar1=-1.0, scalar2=None, op0=ALU.add)
+        theta0_sq = keep.tile([P, TILES], F32)
+        nc.vector.scalar_tensor_tensor(
+            out=theta0_sq[:], in0=theta0[:], scalar=1.0, in1=theta0_m1[:], op0=ALU.add, op1=ALU.mult
+        )
+        theta0_rt = keep.tile([P, TILES], F32)
+        nc.scalar.activation(out=theta0_rt[:], in_=theta0_sq[:], func=ACT.Sqrt)
+        theta0_sum = keep.tile([P, TILES], F32)
+        nc.vector.tensor_tensor(out=theta0_sum[:], in0=theta0[:], in1=theta0_rt[:], op=ALU.add)
+        dist = keep.tile([P, TILES], F32)
+        nc.scalar.activation(out=dist[:], in_=theta0_sum[:], func=ACT.Ln)
+
+        bb = keep.tile([P, 1], F32)
+        t_g = keep.tile([P, 3], F32)
+        t_b = t_g[:, 2:3]
+        t_e = keep.tile([P, 2], F32)
+        t_v = keep.tile([P, 6], F32)
+        t_inv = t_v[:, 0:1]
+        cosh_half = t_v[:, 1:2]
+        sinc2 = t_v[:, 2:3]
+        sinc_quarter = t_v[:, 3:4]
+        one_plus = t_v[:, 5:6]
+        bias_s = keep.tile([P, N], F32)
+
+        def bias_norm():
+            junk_b = junk.tile([P, N], F32, tag="junk_a")
+            nc.vector.scalar_tensor_tensor(
+                out=junk_b[:], in0=bias_bc[:], scalar=1.0, in1=bias_bc[:], op0=ALU.mult, op1=ALU.mult, accum_out=bb[:]
+            )
+            nc.gpsimd.tensor_scalar(out=t_g[:, 0:1], in0=bb[:], scalar1=1e-15, scalar2=None, op0=ALU.max)
+            nc.gpsimd.tensor_tensor(out=t_g[:, 1:2], in0=t_g[:, 0:1], in1=half[:], op=ALU.pow)
+            nc.gpsimd.tensor_scalar(out=t_b, in0=t_g[:, 1:2], scalar1=1e-15, scalar2=15.0, op0=ALU.max, op1=ALU.min)
+
+        def bias_factors():
+            nc.scalar.activation(out=t_e[:, 0:1], in_=t_b, func=ACT.Exp)
+            nc.scalar.activation(out=t_e[:, 1:2], in_=t_b, func=ACT.Exp, scale=-1.0)
+            nc.vector.reciprocal(out=t_inv, in_=t_b)
+            nc.vector.tensor_scalar(
+                out=cosh_half, in0=t_e[:, 0:1], scalar1=t_e[:, 1:2], scalar2=0.25, op0=ALU.add, op1=ALU.mult
+            )
+            nc.vector.scalar_tensor_tensor(
+                out=sinc2, in0=t_e[:, 0:1], scalar=t_e[:, 1:2], in1=t_inv, op0=ALU.subtract, op1=ALU.mult
+            )
+            nc.vector.tensor_scalar(out=sinc_quarter, in0=sinc2, scalar1=0.25, scalar2=None, op0=ALU.mult)
+            nc.vector.scalar_tensor_tensor(
+                out=t_v[:, 4:5], in0=sinc2, scalar=sinc2, in1=bb[:], op0=ALU.mult, op1=ALU.mult
+            )
+            nc.vector.tensor_scalar(out=one_plus, in0=t_v[:, 4:5], scalar1=0.25, scalar2=1.0, op0=ALU.mult, op1=ALU.add)
+
+        def bias_scaled():
+            nc.vector.tensor_scalar(
+                out=bias_s[:], in0=bias_bc[:], scalar1=sinc2, scalar2=0.5, op0=ALU.mult, op1=ALU.mult
+            )
+
+        w_codes = keep.tile([P, PASSES, N], U32, align_bytes=64)
+        w_scales = keep.tile([P, PASSES, N], U8, align_bytes=64)
+        w_words = w_sb[:].bitcast(F32)
+
+        def weight_chunk(c):
+            grouped = []
+            for g in range(PASSES):
+                wt = psum_h.tile([P, 2, W_CHUNK], F32, tag="h", name="wt")
+                for u in range(2):
+                    for b in range(W_CHUNK // P):
+                        nc.tensor.transpose(
+                            wt[:, u, b * P : (b + 1) * P],
+                            w_words[:, c, b, 256 * g + u : 256 * (g + 1) : 2],
+                            ident_f[:],
+                        )
+                w_grouped = wstage.tile([P, W_CHUNK, 4], BF16, align_bytes=64, name="w_grouped")
+                if g == 0:
+                    nc.vector.tensor_copy(out=w_grouped[:].bitcast(F32), in_=wt[:].rearrange("p u n -> p n u"))
+                else:
+                    nc.scalar.copy(out=w_grouped[:].bitcast(F32), in_=wt[:].rearrange("p u n -> p n u"))
+                grouped.append(w_grouped)
+            n_cols = slice(c * W_CHUNK, (c + 1) * W_CHUNK)
+            for g in reversed(range(PASSES)):
+                nc.vector.quantize_mx(
+                    out=w_codes[:, g, n_cols].bitcast(FP8X4),
+                    scales=w_scales[:, g, n_cols],
+                    in_=grouped[g][:].rearrange("p n j -> p (n j)"),
+                )
+
+        tiles = {}
+
+        def sp(t):
+            return x_sb[:, t, 2 : K + 2]
+
+        def norm_of_sp(t):
+            junk_a = junk.tile([P, K], F32, tag="junk_a", name="junk_a")
+            ss = small.tile([P, 1], F32, name="ss")
+            nc.scalar.activation(out=junk_a[:], in_=sp(t), func=ACT.Square, accum_out=ss[:])
+            rn = small.tile([P, 1], F32, name="rn")
+            nc.gpsimd.tensor_tensor(out=rn[:], in0=ss[:], in1=minus_half[:], op=ALU.pow)
+            tiles[("rn", t)] = rn
+
+        def row_scale(t):
+            s_row = small.tile([P, 1], F32, name="s_row")
+            nc.vector.tensor_scalar(
+                out=s_row[:], in0=tiles[("rn", t)][:], scalar1=1e15, scalar2=dist[:, t : t + 1], op0=ALU.min, op1=ALU.mult
+            )
+            tiles[("s", t)] = s_row
+
+        def log_map(t):
+            u_bf = upool.tile([P, K], BF16, name="u_bf")
+            nc.vector.tensor_scalar(out=u_bf[:], in0=sp(t), scalar1=tiles[("s", t)][:], scalar2=None, op0=ALU.mult)
+            ut = psum_t.tile([P, PASSES, 2, P], F32, name="ut")
+            u_words = u_bf[:].bitcast(F32)
+            for g in range(PASSES):
+                for u in range(2):
+                    nc.tensor.transpose(ut[:, g, u, :], u_words[:, 256 * g + u : 256 * (g + 1) : 2], ident_f[:])
+            tiles[("ut", t)] = ut
+
+        def regroup(t):
+            u_grouped = upool.tile([P, PASSES, P, 4], BF16, align_bytes=64, name="u_grouped")
+            nc.scalar.copy(out=u_grouped[:].bitcast(F32), in_=tiles[("ut", t)][:].rearrange("p g u m -> p g m u"))
+            tiles[("ug", t)] = u_grouped
+
+        def quantise(t):
+            u_codes = upool.tile([P, PASSES * P], U32, align_bytes=64, name="u_codes")
+            u_scales = upool.tile([P, PASSES * P], U8, align_bytes=64, name="u_scales")
+            nc.vector.quantize_mx(
+                out=u_codes[:].bitcast(FP8X4),
+                scales=u_scales[:],
+                in_=tiles[("ug", t)][:].rearrange("p g m j -> p (g m j)"),
+            )
+            tiles[("uq", t)] = (u_codes, u_scales)
+
+        def multiply(t, nh):
+            u_codes, u_scales = tiles[("uq", t)]
+            h = psum_h.tile([P, BANK], F32, tag="h", name="h")
+            for g in range(PASSES):
+                nc.tensor.matmul_mx(
+                    out=h[:],
+                    lhsT=u_codes[:, g * P : (g + 1) * P].bitcast(FP8X4),
+                    lhsT_scale=u_scales[:, g * P : (g + 1) * P],
+                    rhs=w_codes[:, g, nh * BANK : (nh + 1) * BANK].bitcast(FP8X4),
+                    rhs_scale=w_scales[:, g, nh * BANK : (nh + 1) * BANK],
+                    start=(g == 0),
+                    stop=(g == PASSES - 1),
+                )
+            tiles[("h", t, nh)] = h
+
+        def norm_of_h(t):
+            hh2 = small.tile([P, BANKS], F32, name="hh2")
+            for nh in range(BANKS):
+                junk_s = junk.tile([P, BANK], F32, name="junk_s")
+                nc.scalar.activation(
+                    out=junk_s[:], in_=tiles[("h", t, nh)][:], func=ACT.Square, accum_out=hh2[:, nh : nh + 1]
+                )
+            hg = small.tile([P, 3], F32, name="hg")
+            nc.gpsimd.tensor_scalar(
+                out=hg[:, 0:1], in0=hh2[:, 0:1], scalar1=hh2[:, 1:2], scalar2=1e-30, op0=ALU.add, op1=ALU.max
+            )
+            nc.gpsimd.tensor_tensor(out=hg[:, 1:2], in0=hg[:, 0:1], in1=minus_half[:], op=ALU.pow)
+            nc.gpsimd.tensor_scalar(
+                out=hg[:, 2:3], in0=hg[:, 0:1], scalar1=hg[:, 1:2], scalar2=15.0, op0=ALU.mult, op1=ALU.min
+            )
+            tiles[("hg", t)] = hg
+
+        def dot_with_bias(t, nh):
+            if nh == 0:
+                tiles[("hb", t)] = small.tile([P, BANKS], F32, name="hb")
+            junk_v = junk.tile([P, BANK], F32, name="junk_v")
+            nc.vector.scalar_tensor_tensor(
+                out=junk_v[:], in0=tiles[("h", t, nh)][:], scalar=sinc_quarter,
+                in1=bias_bc[:, nh * BANK : (nh + 1) * BANK],
+                op0=ALU.mult, op1=ALU.mult, accum_out=tiles[("hb", t)][:, nh : nh + 1],
+            )
+
+        def exponentials(t):
+            theta = tiles[("hg", t)][:, 2:3]
+            ex = small.tile([P, 3], F32, name="ex")
+            nc.scalar.activation(out=ex[:, 0:1], in_=theta, func=ACT.Exp)
+            nc.scalar.activation(out=ex[:, 1:2], in_=theta, func=ACT.Exp, scale=-1.0)
+            nc.scalar.activation(out=ex[:, 2:3], in_=theta, func=ACT.Tanh, scale=0.5)
+            tiles[("ex", t)] = ex
+
+        def row_factor_parts(t):
+            ex = tiles[("ex", t)]
+            hb = tiles[("hb", t)]
+            va = small.tile([P, 7], F32, name="va")
+            nc.vector.scalar_tensor_tensor(
+                out=va[:, 0:1], in0=hb[:, 0:1], scalar=hb[:, 1:2], in1=ex[:, 2:3], op0=ALU.add, op1=ALU.mult
+            )
+            nc.vector.scalar_tensor_tensor(
+                out=va[:, 1:2], in0=ex[:, 0:1], scalar=ex[:, 1:2], in1=tiles[("hg", t)][:, 1:2],
+                op0=ALU.subtract, op1=ALU.mult,
+            )
+            nc.vector.tensor_scalar(
+                out=va[:, 4:5], in0=hb[:, 0:1], scalar1=hb[:, 1:2], scalar2=4.0, op0=ALU.add, op1=ALU.mult
+            )
+            tiles[("va", t)] = va
+
+        def row_factor_sum(t):
+            va = tiles[("va", t)]
+            nc.vector.tensor_scalar(
+                out=va[:, 2:3], in0=va[:, 0:1], scalar1=tiles[("hg", t)][:, 1:2], scalar2=cosh_half,
+                op0=ALU.mult, op1=ALU.add,
+            )
+
+        def row_factor(t):
+            va = tiles[("va", t)]
+            nc.vector.tensor_tensor(out=va[:, 3:4], in0=va[:, 2:3], in1=va[:, 1:2], op=ALU.mult)
+
+        def time_square_inner(t):
+            va = tiles[("va", t)]
+            nc.vector.tensor_scalar(
+                out=va[:, 5:6], in0=tiles[("hg", t)][:, 0:1], scalar1=va[:, 3:4], scalar2=va[:, 4:5],
+                op0=ALU.mult, op1=ALU.add,
+            )
+
+        def time_square(t):
+            va = tiles[("va", t)]
+            nc.vector.tensor_scalar(
+                out=va[:, 6:7], in0=va[:, 5:6], scalar1=va[:, 3:4], scalar2=one_plus, op0=ALU.mult, op1=ALU.add
+            )
+            time_g = small.tile([P, 1], F32, name="time_g")
+            nc.gpsimd.tensor_tensor(out=time_g[:], in0=va[:, 6:7], in1=half[:], op=ALU.pow)
+            tiles[("time", t)] = time_g
+
+        def finish(t, nh):
+            if nh == 0:
+                tiles[("o", t)] = opool.tile([P, N + 1], F32, name="o")
+            nc.vector.scalar_tensor_tensor(
+                out=tiles[("o", t)][:, 1 + nh * BANK : 1 + (nh + 1) * BANK], in0=tiles[("h", t, nh)][:],
+                scalar=tiles[("va", t)][:, 3:4], in1=bias_s[:, nh * BANK : (nh + 1) * BANK],
+                op0=ALU.mult, op1=ALU.add,
+            )
+
+        def store(t):
+            nc.vector.tensor_copy(out=tiles[("o", t)][:, 0:1], in_=tiles[("time", t)][:])
+            nc.sync.dma_start(out=out_rows[:, t, :], in_=tiles[("o", t)][:])
+
+        def live(t):
+            return 0 <= t < TILES
+
+        def period(j):
+            if live(j + AHEAD_NORM):
+                norm_of_sp(j + AHEAD_NORM)
+            if live(j + AHEAD_MATMUL):
+                quantise(j + AHEAD_MATMUL)
+                multiply(j + AHEAD_MATMUL, 0)
+            if live(j - 2):
+                time_square_inner(j - 2)
+                finish(j - 2, 0)
+            if live(j + AHEAD_MATMUL):
+                multiply(j + AHEAD_MATMUL, 1)
+            if live(j + AHEAD_LOG_MAP):
+                row_scale(j + AHEAD_LOG_MAP)
+            if live(j - 2):
+                time_square(j - 2)
+                finish(j - 2, 1)
+            if live(j):
+                norm_of_h(j)
+                dot_with_bias(j, 0)
+            if live(j - 1):
+                exponentials(j - 1)
+                row_factor_parts(j - 1)
+            if live(j):
+                dot_with_bias(j, 1)
+            if live(j - 1):
+                row_factor_sum(j - 1)
+            if live(j + AHEAD_REGROUP):
+                regroup(j + AHEAD_REGROUP)
+            if live(j + AHEAD_LOG_MAP):
+                log_map(j + AHEAD_LOG_MAP)
+            if live(j - 1):
+                row_factor(j - 1)
+            if live(j - 2):
+                store(j - 2)
+
+        period(-4)
+        period(-3)
+        bias_norm()
+        weight_chunk(0)
+        weight_chunk(1)
+        period(-2)
+        bias_factors()
+        weight_chunk(2)
+        weight_chunk(3)
+        period(-1)
+        period(0)
+        bias_scaled()
+        for j in range(1, TILES + 2):
+            period(j)

@@ -1,3 +1,4 @@
+import math
 from contextlib import ExitStack
 
 import concourse.mybir as mybir
@@ -15,7 +16,10 @@ P = 128
 ROWS = 2048
 K = 1024
 N = 1024
+OUT_W = N + 1
 TILES = ROWS // P
+PAIR = 2
+PAIRS = TILES // PAIR
 K_PASS = 512
 PASSES = K // K_PASS
 BANK = 512
@@ -23,10 +27,10 @@ BANKS = N // BANK
 W_CHUNK = 256
 W_CHUNKS = N // W_CHUNK
 X_SLOT = 1040
-AHEAD_NORM = 4
-AHEAD_LOG_MAP = 3
-AHEAD_REGROUP = 2
-AHEAD_MATMUL = 1
+THETA_MAX = 15.0
+EXP_MAX = math.exp(THETA_MAX)
+TANH_MAX = math.tanh(0.5 * THETA_MAX)
+ALIGN = 8
 
 FLOPS = 2 * ROWS * K * N
 
@@ -37,18 +41,18 @@ def tile_hyperboliclinearhyperboloid_kernel(tc, x, weight, bias, out):
         keep = stack.enter_context(tc.tile_pool(name="keep", bufs=1))
         wstage = stack.enter_context(tc.tile_pool(name="wstage", bufs=4))
         upool = stack.enter_context(tc.tile_pool(name="upool", bufs=4))
-        opool = stack.enter_context(tc.tile_pool(name="opool", bufs=4))
         junk = stack.enter_context(tc.tile_pool(name="junk", bufs=3))
-        small = stack.enter_context(tc.tile_pool(name="small", bufs=8))
-        psum_t = stack.enter_context(tc.psum_pool(name="psum_t", bufs=1))
-        psum_h = stack.enter_context(tc.psum_pool(name="psum_h", bufs=7))
+        small = stack.enter_context(tc.tile_pool(name="small", bufs=4))
+        psum_t = stack.enter_context(tc.psum_pool(name="psum_t", bufs=2))
+        psum_h = stack.enter_context(tc.psum_pool(name="psum_h", bufs=6))
         stack.enter_context(tc.manual_schedule())
 
         x_rows = x.rearrange("(p t) c -> p t c", t=TILES)
-        out_rows = out.rearrange("(p t) c -> p t c", t=TILES)
+        out_flat = out.rearrange("(p t) c -> p (t c)", t=TILES)
         w_rows = weight.rearrange("(c b p) k -> p c b k", b=W_CHUNK // P, p=P)
 
         x_head = keep.tile([P, TILES, 16], BF16)
+        bias_row = keep.tile([P, N], BF16)
         bias_bc = keep.tile([P, N], BF16)
         x_sb = keep.tile([P, TILES, X_SLOT], BF16)
         w_sb = keep.tile([P, W_CHUNKS, W_CHUNK // P, K], BF16)
@@ -59,14 +63,16 @@ def tile_hyperboliclinearhyperboloid_kernel(tc, x, weight, bias, out):
         def load_w(c):
             nc.sync.dma_start(out=w_sb[:, c, :, :], in_=w_rows[:, c, :, :])
 
-        nc.sync.dma_start(out=x_head[:], in_=x_rows[:, :, 0:16])
-        load_x(0, 2)
-        nc.sync.dma_start(out=bias_bc[:], in_=bias.rearrange("a b -> (a b)").partition_broadcast(P))
+        nc.vector.memset(bias_row[:], 0.0)
+        nc.scalar.dma_start(out=bias_row[0:1, :], in_=bias)
+        nc.scalar.dma_start(out=x_head[:], in_=x_rows[:, :, 0:16])
+        load_x(0, 1)
+        load_x(1, 2)
         load_w(0)
         load_w(1)
-        load_x(2, 4)
         load_w(2)
         load_w(3)
+        load_x(2, 4)
         load_x(4, 6)
         load_x(6, 8)
         load_x(8, 12)
@@ -74,28 +80,47 @@ def tile_hyperboliclinearhyperboloid_kernel(tc, x, weight, bias, out):
 
         ident_f = keep.tile([P, P], F32)
         make_identity(nc, ident_f[:])
-        half = keep.tile([P, 1], F32)
-        nc.vector.memset(half[:], 0.5)
-        minus_half = keep.tile([P, 1], F32)
+        minus_half = keep.tile([P, PAIR], F32)
         nc.vector.memset(minus_half[:], -0.5)
+        half = keep.tile([P, TILES], F32)
+        nc.vector.memset(half[:], 0.5)
+        ones = keep.tile([P, P], BF16)
+        nc.gpsimd.memset(ones[:], 1.0)
         warm = keep.tile([P, 1], F32)
-        nc.scalar.activation(out=warm[:], in_=half[:], func=ACT.Sqrt)
+        nc.scalar.activation(out=warm[:], in_=half[:, 0:1], func=ACT.Sqrt)
 
-        theta0 = keep.tile([P, TILES], F32)
-        nc.vector.tensor_scalar(out=theta0[:], in0=x_head[:, :, 0], scalar1=1.0 + 1e-7, scalar2=None, op0=ALU.max)
-        theta0_m1 = keep.tile([P, TILES], F32)
-        nc.vector.tensor_scalar(out=theta0_m1[:], in0=theta0[:], scalar1=-1.0, scalar2=None, op0=ALU.add)
-        theta0_sq = keep.tile([P, TILES], F32)
-        nc.vector.scalar_tensor_tensor(
-            out=theta0_sq[:], in0=theta0[:], scalar=1.0, in1=theta0_m1[:], op0=ALU.add, op1=ALU.mult
-        )
-        theta0_rt = keep.tile([P, TILES], F32)
-        nc.scalar.activation(out=theta0_rt[:], in_=theta0_sq[:], func=ACT.Sqrt)
-        theta0_sum = keep.tile([P, TILES], F32)
-        nc.vector.tensor_tensor(out=theta0_sum[:], in0=theta0[:], in1=theta0_rt[:], op=ALU.add)
+        tiles = {}
+
         dist = keep.tile([P, TILES], F32)
-        nc.scalar.activation(out=dist[:], in_=theta0_sum[:], func=ACT.Ln)
 
+        def arccosh_square(times, t0, t1):
+            n = t1 - t0
+            theta0 = small.tile([P, TILES], F32, name="theta0")
+            nc.vector.tensor_scalar(out=theta0[:, 0:n], in0=times, scalar1=1.0 + 1e-7, scalar2=None, op0=ALU.max)
+            theta0_m1 = small.tile([P, TILES], F32, name="theta0_m1")
+            nc.vector.tensor_scalar(out=theta0_m1[:, 0:n], in0=theta0[:, 0:n], scalar1=-1.0, scalar2=None, op0=ALU.add)
+            theta0_sq = small.tile([P, TILES], F32, name="theta0_sq")
+            nc.vector.scalar_tensor_tensor(
+                out=theta0_sq[:, 0:n], in0=theta0[:, 0:n], scalar=1.0, in1=theta0_m1[:, 0:n],
+                op0=ALU.add, op1=ALU.mult,
+            )
+            tiles[("theta0", t0)] = (theta0, theta0_sq)
+
+        def arccosh_root(t0, t1):
+            n = t1 - t0
+            theta0, theta0_sq = tiles[("theta0", t0)]
+            theta0_rt = small.tile([P, TILES], F32, name="theta0_rt")
+            nc.scalar.activation(out=theta0_rt[:, 0:n], in_=theta0_sq[:, 0:n], func=ACT.Sqrt)
+            tiles[("theta0", t0)] = (theta0, theta0_rt)
+
+        def arccosh_log(t0, t1):
+            n = t1 - t0
+            theta0, theta0_rt = tiles[("theta0", t0)]
+            theta0_sum = small.tile([P, TILES], F32, name="theta0_sum")
+            nc.vector.tensor_tensor(out=theta0_sum[:, 0:n], in0=theta0[:, 0:n], in1=theta0_rt[:, 0:n], op=ALU.add)
+            nc.scalar.activation(out=dist[:, t0:t1], in_=theta0_sum[:, 0:n], func=ACT.Ln)
+
+        bb2 = keep.tile([P, BANKS], F32)
         bb = keep.tile([P, 1], F32)
         t_g = keep.tile([P, 3], F32)
         t_b = t_g[:, 2:3]
@@ -104,22 +129,40 @@ def tile_hyperboliclinearhyperboloid_kernel(tc, x, weight, bias, out):
         t_inv = t_v[:, 0:1]
         cosh_half = t_v[:, 1:2]
         sinc2 = t_v[:, 2:3]
-        sinc_quarter = t_v[:, 3:4]
-        one_plus = t_v[:, 5:6]
+        sinc_half = t_v[:, 5:6]
+        one_plus = t_v[:, 4:5]
         bias_s = keep.tile([P, N], F32)
 
-        def bias_norm():
-            junk_b = junk.tile([P, N], F32, tag="junk_a")
-            nc.vector.scalar_tensor_tensor(
-                out=junk_b[:], in0=bias_bc[:], scalar=1.0, in1=bias_bc[:], op0=ALU.mult, op1=ALU.mult, accum_out=bb[:]
-            )
+        def bias_spread():
+            spread = []
+            for nh in range(BANKS):
+                bank = psum_h.tile([P, BANK], F32, tag="h", name="bank")
+                nc.tensor.matmul(
+                    bank[:], lhsT=ones[:], rhs=bias_row[:, nh * BANK : (nh + 1) * BANK], start=True, stop=True
+                )
+                spread.append(bank)
+            for nh in range(BANKS):
+                nc.vector.tensor_copy(out=bias_bc[:, nh * BANK : (nh + 1) * BANK], in_=spread[nh][:])
+                other = BANKS - 1 - nh
+                junk_b = junk.tile([P, BANK], F32, tag="junk_s", name="junk_b")
+                nc.scalar.activation(
+                    out=junk_b[:], in_=spread[other][:], func=ACT.Square, accum_out=bb2[:, other : other + 1]
+                )
+
+        def bias_root():
+            nc.gpsimd.tensor_tensor(out=bb[:], in0=bb2[:, 0:1], in1=bb2[:, 1:2], op=ALU.add)
             nc.gpsimd.tensor_scalar(out=t_g[:, 0:1], in0=bb[:], scalar1=1e-15, scalar2=None, op0=ALU.max)
-            nc.gpsimd.tensor_tensor(out=t_g[:, 1:2], in0=t_g[:, 0:1], in1=half[:], op=ALU.pow)
+            nc.gpsimd.tensor_tensor(out=t_g[:, 1:2], in0=t_g[:, 0:1], in1=half[:, 0:1], op=ALU.pow)
             nc.gpsimd.tensor_scalar(out=t_b, in0=t_g[:, 1:2], scalar1=1e-15, scalar2=15.0, op0=ALU.max, op1=ALU.min)
 
-        def bias_factors():
+        def load_table(func):
+            nc.scalar.activation(out=warm[:], in_=half[:, 0:1], func=func)
+
+        def bias_exps():
             nc.scalar.activation(out=t_e[:, 0:1], in_=t_b, func=ACT.Exp)
             nc.scalar.activation(out=t_e[:, 1:2], in_=t_b, func=ACT.Exp, scale=-1.0)
+
+        def bias_factors():
             nc.vector.reciprocal(out=t_inv, in_=t_b)
             nc.vector.tensor_scalar(
                 out=cosh_half, in0=t_e[:, 0:1], scalar1=t_e[:, 1:2], scalar2=0.25, op0=ALU.add, op1=ALU.mult
@@ -127,11 +170,11 @@ def tile_hyperboliclinearhyperboloid_kernel(tc, x, weight, bias, out):
             nc.vector.scalar_tensor_tensor(
                 out=sinc2, in0=t_e[:, 0:1], scalar=t_e[:, 1:2], in1=t_inv, op0=ALU.subtract, op1=ALU.mult
             )
-            nc.vector.tensor_scalar(out=sinc_quarter, in0=sinc2, scalar1=0.25, scalar2=None, op0=ALU.mult)
+            nc.vector.tensor_scalar(out=sinc_half, in0=sinc2, scalar1=0.25, scalar2=None, op0=ALU.mult)
             nc.vector.scalar_tensor_tensor(
-                out=t_v[:, 4:5], in0=sinc2, scalar=sinc2, in1=bb[:], op0=ALU.mult, op1=ALU.mult
+                out=t_v[:, 3:4], in0=sinc2, scalar=sinc2, in1=bb[:], op0=ALU.mult, op1=ALU.mult
             )
-            nc.vector.tensor_scalar(out=one_plus, in0=t_v[:, 4:5], scalar1=0.25, scalar2=1.0, op0=ALU.mult, op1=ALU.add)
+            nc.vector.tensor_scalar(out=one_plus, in0=t_v[:, 3:4], scalar1=0.25, scalar2=1.0, op0=ALU.mult, op1=ALU.add)
 
         def bias_scaled():
             nc.vector.tensor_scalar(
@@ -141,57 +184,82 @@ def tile_hyperboliclinearhyperboloid_kernel(tc, x, weight, bias, out):
         w_codes = keep.tile([P, PASSES, N], U32, align_bytes=64)
         w_scales = keep.tile([P, PASSES, N], U8, align_bytes=64)
         w_words = w_sb[:].bitcast(F32)
+        w_grouped = {}
 
-        def weight_chunk(c):
-            grouped = []
-            for g in range(PASSES):
-                wt = psum_h.tile([P, 2, W_CHUNK], F32, tag="h", name="wt")
-                for u in range(2):
-                    for b in range(W_CHUNK // P):
-                        nc.tensor.transpose(
-                            wt[:, u, b * P : (b + 1) * P],
-                            w_words[:, c, b, 256 * g + u : 256 * (g + 1) : 2],
-                            ident_f[:],
-                        )
-                w_grouped = wstage.tile([P, W_CHUNK, 4], BF16, align_bytes=64, name="w_grouped")
-                if g == 0:
-                    nc.vector.tensor_copy(out=w_grouped[:].bitcast(F32), in_=wt[:].rearrange("p u n -> p n u"))
-                else:
-                    nc.scalar.copy(out=w_grouped[:].bitcast(F32), in_=wt[:].rearrange("p u n -> p n u"))
-                grouped.append(w_grouped)
+        def weight_turn(c, g):
+            wt = psum_h.tile([P, 2, W_CHUNK], F32, tag="h", name="wt")
+            for u in range(2):
+                for b in range(W_CHUNK // P):
+                    nc.tensor.transpose(
+                        wt[:, u, b * P : (b + 1) * P],
+                        w_words[:, c, b, 256 * g + u : 256 * (g + 1) : 2],
+                        ident_f[:],
+                    )
+            tiles[("wt", c, g)] = wt
+
+        def weight_regroup(c, g, engine):
+            grouped = wstage.tile([P, W_CHUNK, 4], BF16, align_bytes=64, name="grouped")
+            out_words = grouped[:].bitcast(F32)
+            in_words = tiles[("wt", c, g)][:].rearrange("p u n -> p n u")
+            if engine is nc.vector:
+                nc.vector.tensor_copy(out=out_words, in_=in_words)
+            else:
+                nc.scalar.copy(out=out_words, in_=in_words)
+            w_grouped[(c, g)] = grouped
+
+        def weight_quantise(c, g):
             n_cols = slice(c * W_CHUNK, (c + 1) * W_CHUNK)
-            for g in reversed(range(PASSES)):
-                nc.vector.quantize_mx(
-                    out=w_codes[:, g, n_cols].bitcast(FP8X4),
-                    scales=w_scales[:, g, n_cols],
-                    in_=grouped[g][:].rearrange("p n j -> p (n j)"),
-                )
+            nc.vector.quantize_mx(
+                out=w_codes[:, g, n_cols].bitcast(FP8X4),
+                scales=w_scales[:, g, n_cols],
+                in_=w_grouped[(c, g)][:].rearrange("p n j -> p (n j)"),
+            )
 
-        tiles = {}
+        o_all = keep.tile([P, TILES * OUT_W], F32)
+
+        def live(q):
+            return 0 <= q < PAIRS
 
         def sp(t):
             return x_sb[:, t, 2 : K + 2]
 
-        def norm_of_sp(t):
+        def norm_of_sp(q, i, on_vector=False):
             junk_a = junk.tile([P, K], F32, tag="junk_a", name="junk_a")
-            ss = small.tile([P, 1], F32, name="ss")
-            nc.scalar.activation(out=junk_a[:], in_=sp(t), func=ACT.Square, accum_out=ss[:])
-            rn = small.tile([P, 1], F32, name="rn")
-            nc.gpsimd.tensor_tensor(out=rn[:], in0=ss[:], in1=minus_half[:], op=ALU.pow)
-            tiles[("rn", t)] = rn
+            if i == 0:
+                tiles[("ss", q)] = small.tile([P, PAIR], F32, name="ss")
+            total = tiles[("ss", q)][:, i : i + 1]
+            if on_vector:
+                nc.vector.scalar_tensor_tensor(
+                    out=junk_a[:], in0=sp(PAIR * q + i), scalar=1.0, in1=sp(PAIR * q + i),
+                    op0=ALU.mult, op1=ALU.mult, accum_out=total,
+                )
+            else:
+                nc.scalar.activation(out=junk_a[:], in_=sp(PAIR * q + i), func=ACT.Square, accum_out=total)
 
-        def row_scale(t):
-            s_row = small.tile([P, 1], F32, name="s_row")
-            nc.vector.tensor_scalar(
-                out=s_row[:], in0=tiles[("rn", t)][:], scalar1=1e15, scalar2=dist[:, t : t + 1], op0=ALU.min, op1=ALU.mult
+        def root_of_sp(q):
+            rn = small.tile([P, PAIR], F32, name="rn")
+            nc.gpsimd.tensor_tensor(out=rn[:], in0=tiles[("ss", q)][:], in1=minus_half[:], op=ALU.pow)
+            tiles[("rn", q)] = rn
+
+        def row_scale(q):
+            s_row = small.tile([P, PAIR], F32, name="s_row")
+            nc.vector.scalar_tensor_tensor(
+                out=s_row[:], in0=tiles[("rn", q)][:], scalar=1e15, in1=dist[:, PAIR * q : PAIR * (q + 1)],
+                op0=ALU.min, op1=ALU.mult,
             )
-            tiles[("s", t)] = s_row
+            tiles[("s", q)] = s_row
 
-        def log_map(t):
+        def log_map(q, i):
+            t = PAIR * q + i
             u_bf = upool.tile([P, K], BF16, name="u_bf")
-            nc.vector.tensor_scalar(out=u_bf[:], in0=sp(t), scalar1=tiles[("s", t)][:], scalar2=None, op0=ALU.mult)
+            nc.vector.tensor_scalar(
+                out=u_bf[:], in0=sp(t), scalar1=tiles[("s", q)][:, i : i + 1], scalar2=None, op0=ALU.mult
+            )
+            tiles[("u", t)] = u_bf
+
+        def turn(t):
             ut = psum_t.tile([P, PASSES, 2, P], F32, name="ut")
-            u_words = u_bf[:].bitcast(F32)
+            u_words = tiles[("u", t)][:].bitcast(F32)
             for g in range(PASSES):
                 for u in range(2):
                     nc.tensor.transpose(ut[:, g, u, :], u_words[:, 256 * g + u : 256 * (g + 1) : 2], ident_f[:])
@@ -227,146 +295,246 @@ def tile_hyperboliclinearhyperboloid_kernel(tc, x, weight, bias, out):
                 )
             tiles[("h", t, nh)] = h
 
-        def norm_of_h(t):
-            hh2 = small.tile([P, BANKS], F32, name="hh2")
-            for nh in range(BANKS):
-                junk_s = junk.tile([P, BANK], F32, name="junk_s")
-                nc.scalar.activation(
-                    out=junk_s[:], in_=tiles[("h", t, nh)][:], func=ACT.Square, accum_out=hh2[:, nh : nh + 1]
-                )
-            hg = small.tile([P, 3], F32, name="hg")
-            nc.gpsimd.tensor_scalar(
-                out=hg[:, 0:1], in0=hh2[:, 0:1], scalar1=hh2[:, 1:2], scalar2=1e-30, op0=ALU.add, op1=ALU.max
+        def norm_of_h(q, i, nh):
+            if i == 0 and nh == 0:
+                tiles[("hh2", q)] = small.tile([P, PAIR, BANKS], F32, name="hh2")
+            junk_s = junk.tile([P, BANK], F32, name="junk_s")
+            nc.scalar.activation(
+                out=junk_s[:], in_=tiles[("h", PAIR * q + i, nh)][:], func=ACT.Square,
+                accum_out=tiles[("hh2", q)][:, i, nh : nh + 1],
             )
-            nc.gpsimd.tensor_tensor(out=hg[:, 1:2], in0=hg[:, 0:1], in1=minus_half[:], op=ALU.pow)
-            nc.gpsimd.tensor_scalar(
-                out=hg[:, 2:3], in0=hg[:, 0:1], scalar1=hg[:, 1:2], scalar2=15.0, op0=ALU.mult, op1=ALU.min
-            )
-            tiles[("hg", t)] = hg
 
-        def dot_with_bias(t, nh):
-            if nh == 0:
-                tiles[("hb", t)] = small.tile([P, BANKS], F32, name="hb")
+        def roots_of_h(q):
+            hg = small.tile([P, 2, PAIR], F32, name="hg")
+            hh2 = tiles[("hh2", q)]
+            nc.gpsimd.tensor_tensor(out=hg[:, 0, :], in0=hh2[:, :, 0], in1=hh2[:, :, 1], op=ALU.add)
+            nc.gpsimd.tensor_tensor(out=hg[:, 1, :], in0=hg[:, 0, :], in1=half[:, 0:PAIR], op=ALU.pow)
+            tiles[("hg", q)] = hg
+
+        def dot_with_bias(q, i, nh):
+            if i == 0 and nh == 0:
+                tiles[("hb", q)] = small.tile([P, PAIR, BANKS], F32, name="hb")
             junk_v = junk.tile([P, BANK], F32, name="junk_v")
             nc.vector.scalar_tensor_tensor(
-                out=junk_v[:], in0=tiles[("h", t, nh)][:], scalar=sinc_quarter,
+                out=junk_v[:], in0=tiles[("h", PAIR * q + i, nh)][:], scalar=sinc_half,
                 in1=bias_bc[:, nh * BANK : (nh + 1) * BANK],
-                op0=ALU.mult, op1=ALU.mult, accum_out=tiles[("hb", t)][:, nh : nh + 1],
+                op0=ALU.mult, op1=ALU.mult, accum_out=tiles[("hb", q)][:, i, nh : nh + 1],
             )
 
-        def exponentials(t):
-            theta = tiles[("hg", t)][:, 2:3]
-            ex = small.tile([P, 3], F32, name="ex")
-            nc.scalar.activation(out=ex[:, 0:1], in_=theta, func=ACT.Exp)
-            nc.scalar.activation(out=ex[:, 1:2], in_=theta, func=ACT.Exp, scale=-1.0)
-            nc.scalar.activation(out=ex[:, 2:3], in_=theta, func=ACT.Tanh, scale=0.5)
-            tiles[("ex", t)] = ex
+        def exponentials(q):
+            norm = tiles[("hg", q)][:, 1, :]
+            ex = small.tile([P, 3, PAIR], F32, name="ex")
+            nc.scalar.activation(out=ex[:, 0, :], in_=norm, func=ACT.Exp)
+            nc.scalar.activation(out=ex[:, 1, :], in_=norm, func=ACT.Exp, scale=-1.0)
+            nc.scalar.activation(out=ex[:, 2, :], in_=norm, func=ACT.Tanh, scale=0.5)
+            tiles[("ex", q)] = ex
 
-        def row_factor_parts(t):
-            ex = tiles[("ex", t)]
-            hb = tiles[("hb", t)]
-            va = small.tile([P, 7], F32, name="va")
+        def row_factors(q, step):
+            ex = tiles[("ex", q)]
+            hb = tiles[("hb", q)]
+            if step == 0:
+                tiles[("va", q)] = small.tile([P, 7, PAIR], F32, name="va")
+            va = tiles[("va", q)]
+            r_inv = va[:, 6, :]
+            if step == 0:
+                nc.vector.reciprocal(out=r_inv, in_=tiles[("hg", q)][:, 1, :])
+                nc.vector.tensor_tensor(out=va[:, 0, :], in0=hb[:, :, 0], in1=hb[:, :, 1], op=ALU.add)
+                nc.vector.scalar_tensor_tensor(
+                    out=va[:, 1, :], in0=ex[:, 0, :], scalar=EXP_MAX, in1=ex[:, 1, :], op0=ALU.min, op1=ALU.subtract
+                )
+            elif step == 1:
+                nc.vector.scalar_tensor_tensor(
+                    out=va[:, 2, :], in0=ex[:, 2, :], scalar=TANH_MAX, in1=va[:, 0, :], op0=ALU.min, op1=ALU.mult
+                )
+                nc.vector.scalar_tensor_tensor(
+                    out=va[:, 3, :], in0=r_inv, scalar=1e15, in1=va[:, 1, :], op0=ALU.min, op1=ALU.mult
+                )
+            elif step == 2:
+                nc.vector.scalar_tensor_tensor(
+                    out=va[:, 4, :], in0=r_inv, scalar=1e15, in1=va[:, 2, :], op0=ALU.min, op1=ALU.mult
+                )
+            else:
+                nc.vector.scalar_tensor_tensor(
+                    out=va[:, 5, :], in0=va[:, 4, :], scalar=cosh_half, in1=va[:, 3, :], op0=ALU.add, op1=ALU.mult
+                )
+
+        def time_square(q, step):
+            va = tiles[("va", q)]
+            if step == 0:
+                tiles[("vt", q)] = small.tile([P, 3, PAIR], F32, name="vt")
+            vt = tiles[("vt", q)]
+            if step == 0:
+                nc.vector.tensor_tensor(out=vt[:, 0, :], in0=va[:, 5, :], in1=tiles[("hg", q)][:, 0, :], op=ALU.mult)
+            elif step == 1:
+                nc.vector.scalar_tensor_tensor(
+                    out=vt[:, 1, :], in0=va[:, 0, :], scalar=4.0, in1=vt[:, 0, :], op0=ALU.mult, op1=ALU.add
+                )
+            else:
+                for i in range(PAIR):
+                    nc.scalar.activation(
+                        out=vt[:, 2, i : i + 1], in_=vt[:, 1, i : i + 1], func=ACT.Identity,
+                        scale=va[:, 5, i : i + 1], bias=one_plus,
+                    )
+
+        def time_root(q):
+            time_g = small.tile([P, PAIR], F32, name="time_g")
+            nc.gpsimd.tensor_tensor(out=time_g[:], in0=tiles[("vt", q)][:, 2, :], in1=half[:, 0:PAIR], op=ALU.pow)
+            tiles[("time", q)] = time_g
+
+        def finish(q, i, nh):
+            t = PAIR * q + i
+            c0 = OUT_W * t + 1 + nh * BANK
             nc.vector.scalar_tensor_tensor(
-                out=va[:, 0:1], in0=hb[:, 0:1], scalar=hb[:, 1:2], in1=ex[:, 2:3], op0=ALU.add, op1=ALU.mult
-            )
-            nc.vector.scalar_tensor_tensor(
-                out=va[:, 1:2], in0=ex[:, 0:1], scalar=ex[:, 1:2], in1=tiles[("hg", t)][:, 1:2],
-                op0=ALU.subtract, op1=ALU.mult,
-            )
-            nc.vector.tensor_scalar(
-                out=va[:, 4:5], in0=hb[:, 0:1], scalar1=hb[:, 1:2], scalar2=4.0, op0=ALU.add, op1=ALU.mult
-            )
-            tiles[("va", t)] = va
-
-        def row_factor_sum(t):
-            va = tiles[("va", t)]
-            nc.vector.tensor_scalar(
-                out=va[:, 2:3], in0=va[:, 0:1], scalar1=tiles[("hg", t)][:, 1:2], scalar2=cosh_half,
+                out=o_all[:, c0 : c0 + BANK], in0=tiles[("h", t, nh)][:],
+                scalar=tiles[("va", q)][:, 5, i : i + 1], in1=bias_s[:, nh * BANK : (nh + 1) * BANK],
                 op0=ALU.mult, op1=ALU.add,
             )
 
-        def row_factor(t):
-            va = tiles[("va", t)]
-            nc.vector.tensor_tensor(out=va[:, 3:4], in0=va[:, 2:3], in1=va[:, 1:2], op=ALU.mult)
+        def time_column(q):
+            c0 = OUT_W * PAIR * q
+            nc.scalar.copy(out=o_all[:, c0 : c0 + OUT_W + 1 : OUT_W], in_=tiles[("time", q)][:])
 
-        def time_square_inner(t):
-            va = tiles[("va", t)]
-            nc.vector.tensor_scalar(
-                out=va[:, 5:6], in0=tiles[("hg", t)][:, 0:1], scalar1=va[:, 3:4], scalar2=va[:, 4:5],
-                op0=ALU.mult, op1=ALU.add,
-            )
+        def store_to(t):
+            return OUT_W * t // ALIGN * ALIGN
 
-        def time_square(t):
-            va = tiles[("va", t)]
-            nc.vector.tensor_scalar(
-                out=va[:, 6:7], in0=va[:, 5:6], scalar1=va[:, 3:4], scalar2=one_plus, op0=ALU.mult, op1=ALU.add
-            )
-            time_g = small.tile([P, 1], F32, name="time_g")
-            nc.gpsimd.tensor_tensor(out=time_g[:], in0=va[:, 6:7], in1=half[:], op=ALU.pow)
-            tiles[("time", t)] = time_g
+        def store(t0, t1):
+            cols = slice(store_to(t0), store_to(t1))
+            nc.sync.dma_start(out=out_flat[:, cols], in_=o_all[:, cols])
 
-        def finish(t, nh):
-            if nh == 0:
-                tiles[("o", t)] = opool.tile([P, N + 1], F32, name="o")
-            nc.vector.scalar_tensor_tensor(
-                out=tiles[("o", t)][:, 1 + nh * BANK : 1 + (nh + 1) * BANK], in0=tiles[("h", t, nh)][:],
-                scalar=tiles[("va", t)][:, 3:4], in1=bias_s[:, nh * BANK : (nh + 1) * BANK],
-                op0=ALU.mult, op1=ALU.add,
-            )
+        def period(q):
+            if live(q):
+                row_factors(q, 0)
+            if live(q + 3):
+                norm_of_sp(q + 3, 0)
+            if live(q + 1):
+                quantise(PAIR * (q + 1))
+                multiply(PAIR * (q + 1), 0)
+                norm_of_h(q + 1, 0, 0)
+                multiply(PAIR * (q + 1), 1)
+                norm_of_h(q + 1, 0, 1)
+            if live(q):
+                row_factors(q, 1)
+            if live(q + 1):
+                quantise(PAIR * (q + 1) + 1)
+            if live(q):
+                row_factors(q, 2)
+            if live(q + 2):
+                row_scale(q + 2)
+            if live(q):
+                row_factors(q, 3)
+            if live(q + 2):
+                log_map(q + 2, 0)
+                turn(PAIR * (q + 2))
+                log_map(q + 2, 1)
+                turn(PAIR * (q + 2) + 1)
+            if live(q - 1):
+                time_square(q - 1, 2)
+                time_root(q - 1)
+            if live(q):
+                finish(q, 0, 0)
+            if live(q + 1):
+                multiply(PAIR * (q + 1) + 1, 0)
+                norm_of_h(q + 1, 1, 0)
+            if live(q):
+                time_square(q, 0)
+                finish(q, 0, 1)
+            if live(q + 1):
+                multiply(PAIR * (q + 1) + 1, 1)
+                norm_of_h(q + 1, 1, 1)
+                roots_of_h(q + 1)
+            if live(q):
+                time_square(q, 1)
+                finish(q, 1, 0)
+                finish(q, 1, 1)
+            if live(q + 3):
+                norm_of_sp(q + 3, 1)
+                root_of_sp(q + 3)
+            if live(q + 1):
+                exponentials(q + 1)
+            if live(q + 2):
+                regroup(PAIR * (q + 2))
+                regroup(PAIR * (q + 2) + 1)
+            for i in range(PAIR):
+                for nh in range(BANKS):
+                    if live(q + 1):
+                        dot_with_bias(q + 1, i, nh)
+            if live(q - 1):
+                time_column(q - 1)
+                store(PAIR * (q - 1), PAIR * q)
 
-        def store(t):
-            nc.vector.tensor_copy(out=tiles[("o", t)][:, 0:1], in_=tiles[("time", t)][:])
-            nc.sync.dma_start(out=out_rows[:, t, :], in_=tiles[("o", t)][:])
-
-        def live(t):
-            return 0 <= t < TILES
-
-        def period(j):
-            if live(j + AHEAD_NORM):
-                norm_of_sp(j + AHEAD_NORM)
-            if live(j + AHEAD_MATMUL):
-                quantise(j + AHEAD_MATMUL)
-                multiply(j + AHEAD_MATMUL, 0)
-            if live(j - 2):
-                time_square_inner(j - 2)
-                finish(j - 2, 0)
-            if live(j + AHEAD_MATMUL):
-                multiply(j + AHEAD_MATMUL, 1)
-            if live(j + AHEAD_LOG_MAP):
-                row_scale(j + AHEAD_LOG_MAP)
-            if live(j - 2):
-                time_square(j - 2)
-                finish(j - 2, 1)
-            if live(j):
-                norm_of_h(j)
-                dot_with_bias(j, 0)
-            if live(j - 1):
-                exponentials(j - 1)
-                row_factor_parts(j - 1)
-            if live(j):
-                dot_with_bias(j, 1)
-            if live(j - 1):
-                row_factor_sum(j - 1)
-            if live(j + AHEAD_REGROUP):
-                regroup(j + AHEAD_REGROUP)
-            if live(j + AHEAD_LOG_MAP):
-                log_map(j + AHEAD_LOG_MAP)
-            if live(j - 1):
-                row_factor(j - 1)
-            if live(j - 2):
-                store(j - 2)
-
-        period(-4)
-        period(-3)
-        bias_norm()
-        weight_chunk(0)
-        weight_chunk(1)
-        period(-2)
+        V, S = nc.vector, nc.scalar
+        norm_of_sp(0, 0)
+        bias_spread()
+        norm_of_sp(0, 1, on_vector=True)
+        arccosh_square(x_head[:, :, 0], 0, TILES)
+        arccosh_root(0, TILES)
+        load_table(ACT.Ln)
+        root_of_sp(0)
+        bias_root()
+        weight_turn(0, 0)
+        weight_turn(0, 1)
+        weight_regroup(0, 0, V)
+        arccosh_log(0, TILES)
+        load_table(ACT.Exp)
+        weight_regroup(0, 1, V)
+        weight_turn(1, 0)
+        weight_turn(1, 1)
+        weight_regroup(1, 0, V)
+        row_scale(0)
+        weight_quantise(0, 0)
+        log_map(0, 0)
+        turn(0)
+        log_map(0, 1)
+        turn(1)
+        bias_exps()
+        regroup(0)
+        regroup(1)
+        weight_quantise(0, 1)
+        weight_regroup(1, 1, V)
+        weight_quantise(1, 0)
+        weight_turn(2, 0)
+        weight_turn(2, 1)
+        weight_turn(3, 0)
         bias_factors()
-        weight_chunk(2)
-        weight_chunk(3)
-        period(-1)
-        period(0)
+        weight_quantise(1, 1)
+        weight_regroup(2, 0, S)
+        quantise(0)
+        multiply(0, 0)
+        quantise(1)
+        multiply(1, 0)
+        weight_turn(3, 1)
+        weight_regroup(2, 1, V)
+        norm_of_sp(1, 0)
+        weight_quantise(2, 0)
+        weight_regroup(3, 0, V)
+        norm_of_h(0, 0, 0)
+        weight_quantise(2, 1)
+        norm_of_h(0, 1, 0)
+        dot_with_bias(0, 0, 0)
+        weight_regroup(3, 1, S)
+        weight_quantise(3, 0)
+        dot_with_bias(0, 1, 0)
+        weight_quantise(3, 1)
+        multiply(0, 1)
+        multiply(1, 1)
+        norm_of_sp(1, 1)
+        root_of_sp(1)
+        norm_of_h(0, 0, 1)
+        norm_of_h(0, 1, 1)
+        roots_of_h(0)
         bias_scaled()
-        for j in range(1, TILES + 2):
-            period(j)
+        dot_with_bias(0, 0, 1)
+        row_scale(1)
+        dot_with_bias(0, 1, 1)
+        log_map(1, 0)
+        turn(2)
+        log_map(1, 1)
+        turn(3)
+        norm_of_sp(2, 0)
+        exponentials(0)
+        regroup(2)
+        regroup(3)
+        norm_of_sp(2, 1)
+        root_of_sp(2)
+        for q in range(PAIRS + 1):
+            period(q)

@@ -43,8 +43,8 @@ def tile_hyperboliclinearhyperboloid_kernel(tc, x, weight, bias, out):
         upool = stack.enter_context(tc.tile_pool(name="upool", bufs=4))
         junk = stack.enter_context(tc.tile_pool(name="junk", bufs=3))
         small = stack.enter_context(tc.tile_pool(name="small", bufs=4))
-        psum_t = stack.enter_context(tc.psum_pool(name="psum_t", bufs=2))
-        psum_h = stack.enter_context(tc.psum_pool(name="psum_h", bufs=6))
+        psum_t = stack.enter_context(tc.psum_pool(name="psum_t", bufs=1))
+        psum_h = stack.enter_context(tc.psum_pool(name="psum_h", bufs=7))
         stack.enter_context(tc.manual_schedule())
 
         x_rows = x.rearrange("(p t) c -> p t c", t=TILES)
@@ -63,9 +63,9 @@ def tile_hyperboliclinearhyperboloid_kernel(tc, x, weight, bias, out):
         def load_w(c):
             nc.sync.dma_start(out=w_sb[:, c, :, :], in_=w_rows[:, c, :, :])
 
-        nc.vector.memset(bias_row[:], 0.0)
-        nc.scalar.dma_start(out=bias_row[0:1, :], in_=bias)
+        nc.gpsimd.memset(bias_row[:].bitcast(F32), 0.0)
         nc.scalar.dma_start(out=x_head[:], in_=x_rows[:, :, 0:16])
+        nc.sync.dma_start(out=bias_row[0:1, :], in_=bias)
         load_x(0, 1)
         load_x(1, 2)
         load_w(0)
@@ -113,12 +113,15 @@ def tile_hyperboliclinearhyperboloid_kernel(tc, x, weight, bias, out):
             nc.scalar.activation(out=theta0_rt[:, 0:n], in_=theta0_sq[:, 0:n], func=ACT.Sqrt)
             tiles[("theta0", t0)] = (theta0, theta0_rt)
 
-        def arccosh_log(t0, t1):
+        def arccosh_sum(t0, t1):
             n = t1 - t0
             theta0, theta0_rt = tiles[("theta0", t0)]
             theta0_sum = small.tile([P, TILES], F32, name="theta0_sum")
             nc.vector.tensor_tensor(out=theta0_sum[:, 0:n], in0=theta0[:, 0:n], in1=theta0_rt[:, 0:n], op=ALU.add)
-            nc.scalar.activation(out=dist[:, t0:t1], in_=theta0_sum[:, 0:n], func=ACT.Ln)
+            tiles[("theta0", t0)] = theta0_sum
+
+        def arccosh_log(t0, t1):
+            nc.scalar.activation(out=dist[:, t0:t1], in_=tiles[("theta0", t0)][:, 0 : t1 - t0], func=ACT.Ln)
 
         bb2 = keep.tile([P, BANKS], F32)
         bb = keep.tile([P, 1], F32)
@@ -141,13 +144,16 @@ def tile_hyperboliclinearhyperboloid_kernel(tc, x, weight, bias, out):
                     bank[:], lhsT=ones[:], rhs=bias_row[:, nh * BANK : (nh + 1) * BANK], start=True, stop=True
                 )
                 spread.append(bank)
-            for nh in range(BANKS):
-                nc.vector.tensor_copy(out=bias_bc[:, nh * BANK : (nh + 1) * BANK], in_=spread[nh][:])
-                other = BANKS - 1 - nh
-                junk_b = junk.tile([P, BANK], F32, tag="junk_s", name="junk_b")
-                nc.scalar.activation(
-                    out=junk_b[:], in_=spread[other][:], func=ACT.Square, accum_out=bb2[:, other : other + 1]
-                )
+            tiles["spread"] = spread
+
+        def bias_copy(nh):
+            nc.vector.tensor_copy(out=bias_bc[:, nh * BANK : (nh + 1) * BANK], in_=tiles["spread"][nh][:])
+
+        def bias_square(nh):
+            junk_b = junk.tile([P, BANK], F32, tag="junk_s", name="junk_b")
+            nc.scalar.activation(
+                out=junk_b[:], in_=tiles["spread"][nh][:], func=ACT.Square, accum_out=bb2[:, nh : nh + 1]
+            )
 
         def bias_root():
             nc.gpsimd.tensor_tensor(out=bb[:], in0=bb2[:, 0:1], in1=bb2[:, 1:2], op=ALU.add)
@@ -402,139 +408,174 @@ def tile_hyperboliclinearhyperboloid_kernel(tc, x, weight, bias, out):
             nc.sync.dma_start(out=out_flat[:, cols], in_=o_all[:, cols])
 
         def period(q):
-            if live(q):
-                row_factors(q, 0)
-            if live(q + 3):
-                norm_of_sp(q + 3, 0)
+            last = q == PAIRS - 1
+            if last:
+                time_square(q, 0)
+                time_square(q, 1)
             if live(q + 1):
-                quantise(PAIR * (q + 1))
-                multiply(PAIR * (q + 1), 0)
                 norm_of_h(q + 1, 0, 0)
-                multiply(PAIR * (q + 1), 1)
                 norm_of_h(q + 1, 0, 1)
-            if live(q):
-                row_factors(q, 1)
-            if live(q + 1):
-                quantise(PAIR * (q + 1) + 1)
-            if live(q):
-                row_factors(q, 2)
-            if live(q + 2):
-                row_scale(q + 2)
-            if live(q):
-                row_factors(q, 3)
-            if live(q + 2):
-                log_map(q + 2, 0)
-                turn(PAIR * (q + 2))
-                log_map(q + 2, 1)
-                turn(PAIR * (q + 2) + 1)
             if live(q - 1):
                 time_square(q - 1, 2)
                 time_root(q - 1)
-            if live(q):
-                finish(q, 0, 0)
+            if last:
+                time_square(q, 2)
+                time_root(q)
+            if live(q + 3):
+                root_of_sp(q + 3)
             if live(q + 1):
-                multiply(PAIR * (q + 1) + 1, 0)
                 norm_of_h(q + 1, 1, 0)
-            if live(q):
-                time_square(q, 0)
-                finish(q, 0, 1)
+            if live(q + 2):
+                regroup(PAIR * (q + 2))
+            finish(q, 0, 0)
             if live(q + 1):
                 multiply(PAIR * (q + 1) + 1, 1)
                 norm_of_h(q + 1, 1, 1)
                 roots_of_h(q + 1)
-            if live(q):
-                time_square(q, 1)
-                finish(q, 1, 0)
-                finish(q, 1, 1)
-            if live(q + 3):
-                norm_of_sp(q + 3, 1)
-                root_of_sp(q + 3)
+            if live(q + 2):
+                turn(PAIR * (q + 2) + 1)
+            finish(q, 0, 1)
+            if live(q - 1) and last:
+                time_column(q - 1)
+                store(PAIR * (q - 1), PAIR * q)
+                time_column(q)
+                store(PAIR * q, PAIR * q + 1)
+            finish(q, 1, 0)
+            finish(q, 1, 1)
+            if last:
+                store(PAIR * q + 1, PAIR * (q + 1))
+            if live(q + 4):
+                norm_of_sp(q + 4, 0)
+            if live(q + 2):
+                regroup(PAIR * (q + 2) + 1)
             if live(q + 1):
                 exponentials(q + 1)
-            if live(q + 2):
-                regroup(PAIR * (q + 2))
-                regroup(PAIR * (q + 2) + 1)
-            for i in range(PAIR):
-                for nh in range(BANKS):
-                    if live(q + 1):
+                for i in range(PAIR):
+                    for nh in range(BANKS):
                         dot_with_bias(q + 1, i, nh)
-            if live(q - 1):
+            if live(q + 4):
+                norm_of_sp(q + 4, 1)
+            if live(q + 3):
+                row_scale(q + 3)
+            if live(q + 2):
+                quantise(PAIR * (q + 2))
+                multiply(PAIR * (q + 2), 0)
+                multiply(PAIR * (q + 2), 1)
+            if live(q + 1):
+                row_factors(q + 1, 0)
+                time_square(q, 0)
+            if live(q + 3):
+                log_map(q + 3, 0)
+                turn(PAIR * (q + 3))
+            if live(q + 1):
+                row_factors(q + 1, 1)
+                time_square(q, 1)
+            if live(q + 3):
+                log_map(q + 3, 1)
+            if live(q + 1):
+                row_factors(q + 1, 2)
+            if live(q + 2):
+                quantise(PAIR * (q + 2) + 1)
+                multiply(PAIR * (q + 2) + 1, 0)
+            if live(q + 1):
+                row_factors(q + 1, 3)
+            if live(q - 1) and not last:
                 time_column(q - 1)
                 store(PAIR * (q - 1), PAIR * q)
 
         V, S = nc.vector, nc.scalar
-        norm_of_sp(0, 0)
         bias_spread()
-        norm_of_sp(0, 1, on_vector=True)
+        norm_of_sp(0, 0)
+        bias_copy(0)
+        bias_square(1)
+        bias_square(0)
         arccosh_square(x_head[:, :, 0], 0, TILES)
         arccosh_root(0, TILES)
         load_table(ACT.Ln)
-        root_of_sp(0)
-        bias_root()
-        weight_turn(0, 0)
-        weight_turn(0, 1)
-        weight_regroup(0, 0, V)
+        norm_of_sp(0, 1, on_vector=True)
+        arccosh_sum(0, TILES)
         arccosh_log(0, TILES)
         load_table(ACT.Exp)
-        weight_regroup(0, 1, V)
+        root_of_sp(0)
+        bias_root()
+        bias_copy(1)
+        weight_turn(0, 0)
+        weight_turn(0, 1)
         weight_turn(1, 0)
         weight_turn(1, 1)
-        weight_regroup(1, 0, V)
+        weight_regroup(0, 0, V)
         row_scale(0)
-        weight_quantise(0, 0)
+        weight_regroup(0, 1, V)
         log_map(0, 0)
         turn(0)
         log_map(0, 1)
-        turn(1)
-        bias_exps()
+        weight_regroup(1, 0, V)
         regroup(0)
-        regroup(1)
-        weight_quantise(0, 1)
-        weight_regroup(1, 1, V)
-        weight_quantise(1, 0)
         weight_turn(2, 0)
         weight_turn(2, 1)
-        weight_turn(3, 0)
-        bias_factors()
+        turn(1)
+        weight_regroup(1, 1, V)
+        weight_quantise(0, 0)
+        weight_quantise(0, 1)
+        weight_quantise(1, 0)
         weight_quantise(1, 1)
-        weight_regroup(2, 0, S)
         quantise(0)
         multiply(0, 0)
+        weight_turn(3, 0)
+        weight_turn(3, 1)
+        bias_exps()
+        weight_regroup(2, 0, S)
+        regroup(1)
+        bias_factors()
+        weight_regroup(2, 1, V)
         quantise(1)
         multiply(1, 0)
-        weight_turn(3, 1)
-        weight_regroup(2, 1, V)
         norm_of_sp(1, 0)
+        norm_of_h(0, 0, 0)
         weight_quantise(2, 0)
         weight_regroup(3, 0, V)
-        norm_of_h(0, 0, 0)
         weight_quantise(2, 1)
-        norm_of_h(0, 1, 0)
         dot_with_bias(0, 0, 0)
-        weight_regroup(3, 1, S)
+        norm_of_sp(1, 1)
+        root_of_sp(1)
+        norm_of_h(0, 1, 0)
+        weight_regroup(3, 1, V)
         weight_quantise(3, 0)
-        dot_with_bias(0, 1, 0)
         weight_quantise(3, 1)
         multiply(0, 1)
         multiply(1, 1)
-        norm_of_sp(1, 1)
-        root_of_sp(1)
-        norm_of_h(0, 0, 1)
-        norm_of_h(0, 1, 1)
-        roots_of_h(0)
-        bias_scaled()
-        dot_with_bias(0, 0, 1)
         row_scale(1)
-        dot_with_bias(0, 1, 1)
+        dot_with_bias(0, 1, 0)
         log_map(1, 0)
         turn(2)
         log_map(1, 1)
-        turn(3)
         norm_of_sp(2, 0)
-        exponentials(0)
-        regroup(2)
-        regroup(3)
+        norm_of_h(0, 0, 1)
+        norm_of_h(0, 1, 1)
+        roots_of_h(0)
         norm_of_sp(2, 1)
         root_of_sp(2)
-        for q in range(PAIRS + 1):
+        regroup(2)
+        turn(3)
+        bias_scaled()
+        dot_with_bias(0, 0, 1)
+        dot_with_bias(0, 1, 1)
+        quantise(2)
+        multiply(2, 0)
+        multiply(2, 1)
+        exponentials(0)
+        regroup(3)
+        row_factors(0, 0)
+        row_factors(0, 1)
+        quantise(3)
+        multiply(3, 0)
+        row_factors(0, 2)
+        row_scale(2)
+        row_factors(0, 3)
+        log_map(2, 0)
+        turn(4)
+        log_map(2, 1)
+        norm_of_sp(3, 0)
+        norm_of_sp(3, 1)
+        for q in range(PAIRS):
             period(q)

@@ -192,8 +192,16 @@ def tile_hyperboliclinearhyperboloid_kernel(tc, x, weight, bias, out):
         w_words = w_sb[:].bitcast(F32)
         w_grouped = {}
 
-        def weight_turn(c, g):
+        def keep_clock(bank):
+            for nh in range(BANKS):
+                nc.tensor.matmul(
+                    bank, lhsT=ones[:], rhs=bias_row[:, nh * BANK : (nh + 1) * BANK], start=True, stop=True
+                )
+
+        def weight_turn(c, g, clock=False):
             wt = psum_h.tile([P, 2, W_CHUNK], F32, tag="h", name="wt")
+            if clock:
+                keep_clock(wt[:].rearrange("p u n -> p (u n)"))
             for u in range(2):
                 for b in range(W_CHUNK // P):
                     nc.tensor.transpose(
@@ -263,8 +271,10 @@ def tile_hyperboliclinearhyperboloid_kernel(tc, x, weight, bias, out):
             )
             tiles[("u", t)] = u_bf
 
-        def turn(t):
+        def turn(t, clock=False):
             ut = psum_t.tile([P, PASSES, 2, P], F32, name="ut")
+            if clock:
+                keep_clock(ut[:].rearrange("p g u m -> p (g u m)"))
             u_words = tiles[("u", t)][:].bitcast(F32)
             for g in range(PASSES):
                 for u in range(2):
@@ -433,7 +443,7 @@ def tile_hyperboliclinearhyperboloid_kernel(tc, x, weight, bias, out):
                 norm_of_h(q + 1, 1, 1)
                 roots_of_h(q + 1)
             if live(q + 2):
-                turn(PAIR * (q + 2) + 1)
+                turn(PAIR * (q + 2) + 1, clock=True)
             finish(q, 0, 1)
             if live(q - 1) and last:
                 time_column(q - 1)
@@ -499,9 +509,9 @@ def tile_hyperboliclinearhyperboloid_kernel(tc, x, weight, bias, out):
         root_of_sp(0)
         bias_root()
         bias_copy(1)
-        weight_turn(0, 0)
+        weight_turn(0, 0, clock=True)
         weight_turn(0, 1)
-        weight_turn(1, 0)
+        weight_turn(1, 0, clock=True)
         weight_turn(1, 1)
         weight_regroup(0, 0, V)
         row_scale(0)
@@ -511,7 +521,7 @@ def tile_hyperboliclinearhyperboloid_kernel(tc, x, weight, bias, out):
         log_map(0, 1)
         weight_regroup(1, 0, V)
         regroup(0)
-        weight_turn(2, 0)
+        weight_turn(2, 0, clock=True)
         weight_turn(2, 1)
         turn(1)
         weight_regroup(1, 1, V)

@@ -30,6 +30,7 @@ X_SLOT = 1040
 THETA_MAX = 15.0
 EXP_MAX = math.exp(THETA_MAX)
 TANH_MAX = math.tanh(0.5 * THETA_MAX)
+BEHIND = 3
 ALIGN = 8
 
 FLOPS = 2 * ROWS * K * N
@@ -84,6 +85,9 @@ def tile_hyperboliclinearhyperboloid_kernel(tc, x, weight, bias, out):
         nc.vector.memset(minus_half[:], -0.5)
         half = keep.tile([P, TILES], F32)
         nc.vector.memset(half[:], 0.5)
+        powers = keep.tile([P, 2, PAIR], F32)
+        nc.vector.memset(powers[:, 0, :], 0.5)
+        nc.vector.memset(powers[:, 1, :], -0.5)
         ones = keep.tile([P, P], BF16)
         nc.gpsimd.memset(ones[:], 1.0)
         warm = keep.tile([P, 1], F32)
@@ -234,14 +238,17 @@ def tile_hyperboliclinearhyperboloid_kernel(tc, x, weight, bias, out):
         def live(q):
             return 0 <= q < PAIRS
 
+        def squares_of(q):
+            if ("squares", q) not in tiles:
+                tiles[("squares", q)] = small.tile([P, 2, PAIR], F32, name="squares")
+            return tiles[("squares", q)]
+
         def sp(t):
             return x_sb[:, t, 2 : K + 2]
 
         def norm_of_sp(q, i, on_vector=False):
             junk_a = junk.tile([P, K], F32, tag="junk_a", name="junk_a")
-            if i == 0:
-                tiles[("ss", q)] = small.tile([P, PAIR], F32, name="ss")
-            total = tiles[("ss", q)][:, i : i + 1]
+            total = squares_of(q)[:, 1, i : i + 1]
             if on_vector:
                 nc.vector.scalar_tensor_tensor(
                     out=junk_a[:], in0=sp(PAIR * q + i), scalar=1.0, in1=sp(PAIR * q + i),
@@ -250,15 +257,18 @@ def tile_hyperboliclinearhyperboloid_kernel(tc, x, weight, bias, out):
             else:
                 nc.scalar.activation(out=junk_a[:], in_=sp(PAIR * q + i), func=ACT.Square, accum_out=total)
 
-        def root_of_sp(q):
-            rn = small.tile([P, PAIR], F32, name="rn")
-            nc.gpsimd.tensor_tensor(out=rn[:], in0=tiles[("ss", q)][:], in1=minus_half[:], op=ALU.pow)
-            tiles[("rn", q)] = rn
+        def roots(q):
+            which = slice(0 if live(q - BEHIND) else 1, 2 if live(q) else 1)
+            both = small.tile([P, 2, PAIR], F32, name="both")
+            nc.gpsimd.tensor_tensor(
+                out=both[:, which, :], in0=squares_of(q)[:, which, :], in1=powers[:, which, :], op=ALU.pow
+            )
+            tiles[("roots", q)] = both
 
         def row_scale(q):
             s_row = small.tile([P, PAIR], F32, name="s_row")
             nc.vector.scalar_tensor_tensor(
-                out=s_row[:], in0=tiles[("rn", q)][:], scalar=1e15, in1=dist[:, PAIR * q : PAIR * (q + 1)],
+                out=s_row[:], in0=tiles[("roots", q)][:, 1, :], scalar=1e15, in1=dist[:, PAIR * q : PAIR * (q + 1)],
                 op0=ALU.min, op1=ALU.mult,
             )
             tiles[("s", q)] = s_row
@@ -377,7 +387,7 @@ def tile_hyperboliclinearhyperboloid_kernel(tc, x, weight, bias, out):
         def time_square(q, step):
             va = tiles[("va", q)]
             if step == 0:
-                tiles[("vt", q)] = small.tile([P, 3, PAIR], F32, name="vt")
+                tiles[("vt", q)] = small.tile([P, 2, PAIR], F32, name="vt")
             vt = tiles[("vt", q)]
             if step == 0:
                 nc.vector.tensor_tensor(out=vt[:, 0, :], in0=va[:, 5, :], in1=tiles[("hg", q)][:, 0, :], op=ALU.mult)
@@ -388,14 +398,10 @@ def tile_hyperboliclinearhyperboloid_kernel(tc, x, weight, bias, out):
             else:
                 for i in range(PAIR):
                     nc.scalar.activation(
-                        out=vt[:, 2, i : i + 1], in_=vt[:, 1, i : i + 1], func=ACT.Identity,
+                        out=squares_of(q + BEHIND)[:, 0, i : i + 1], in_=vt[:, 1, i : i + 1], func=ACT.Identity,
                         scale=va[:, 5, i : i + 1], bias=one_plus,
                     )
 
-        def time_root(q):
-            time_g = small.tile([P, PAIR], F32, name="time_g")
-            nc.gpsimd.tensor_tensor(out=time_g[:], in0=tiles[("vt", q)][:, 2, :], in1=half[:, 0:PAIR], op=ALU.pow)
-            tiles[("time", q)] = time_g
 
         def finish(q, i, nh):
             t = PAIR * q + i
@@ -408,54 +414,58 @@ def tile_hyperboliclinearhyperboloid_kernel(tc, x, weight, bias, out):
 
         def time_column(q):
             c0 = OUT_W * PAIR * q
-            nc.scalar.copy(out=o_all[:, c0 : c0 + OUT_W + 1 : OUT_W], in_=tiles[("time", q)][:])
+            for i in range(PAIR):
+                nc.scalar.copy(
+                    out=o_all[:, c0 + i * OUT_W : c0 + i * OUT_W + 1], in_=tiles[("roots", q + BEHIND)][:, 0, i : i + 1]
+                )
 
-        def store_to(t):
-            return OUT_W * t // ALIGN * ALIGN
-
-        def store(t0, t1):
-            cols = slice(store_to(t0), store_to(t1))
+        def store(c0, c1):
+            cols = slice(c0 // ALIGN * ALIGN, c1 // ALIGN * ALIGN)
             nc.sync.dma_start(out=out_flat[:, cols], in_=o_all[:, cols])
 
         def period(q):
             last = q == PAIRS - 1
-            if last:
-                time_square(q, 0)
-                time_square(q, 1)
+            c0 = OUT_W * PAIR * q
             if live(q + 1):
                 norm_of_h(q + 1, 0, 0)
                 norm_of_h(q + 1, 0, 1)
-            if live(q - 1):
-                time_square(q - 1, 2)
-                time_root(q - 1)
-            if last:
-                time_square(q, 2)
-                time_root(q)
-            if live(q + 3):
-                root_of_sp(q + 3)
-            if live(q + 1):
                 norm_of_h(q + 1, 1, 0)
-            if live(q + 2):
-                regroup(PAIR * (q + 2))
+            if last:
+                time_square(q, 0)
+                time_square(q, 1)
+                time_square(q, 2)
+                roots(q + BEHIND)
+                time_column(q)
             finish(q, 0, 0)
             if live(q + 1):
                 multiply(PAIR * (q + 1) + 1, 1)
+            if not last:
+                time_square(q, 0)
+            finish(q, 0, 1)
+            if not last:
+                time_square(q, 1)
+                time_square(q, 2)
+                roots(q + BEHIND)
+            if live(q + 2):
+                regroup(PAIR * (q + 2))
+            if live(q + 1):
                 norm_of_h(q + 1, 1, 1)
                 roots_of_h(q + 1)
             if live(q + 2):
                 turn(PAIR * (q + 2) + 1, clock=True)
-            finish(q, 0, 1)
-            if live(q - 1) and last:
-                time_column(q - 1)
-                store(PAIR * (q - 1), PAIR * q)
-                time_column(q)
-                store(PAIR * q, PAIR * q + 1)
+            if last:
+                store(c0, c0 + OUT_W)
             finish(q, 1, 0)
+            if last:
+                store(c0 + OUT_W, c0 + OUT_W + 1 + BANK)
             finish(q, 1, 1)
             if last:
-                store(PAIR * q + 1, PAIR * (q + 1))
+                store(c0 + OUT_W + 1 + BANK, c0 + PAIR * OUT_W)
             if live(q + 4):
                 norm_of_sp(q + 4, 0)
+            if not last:
+                time_column(q)
+                store(c0, c0 + PAIR * OUT_W)
             if live(q + 2):
                 regroup(PAIR * (q + 2) + 1)
             if live(q + 1):
@@ -465,33 +475,28 @@ def tile_hyperboliclinearhyperboloid_kernel(tc, x, weight, bias, out):
                         dot_with_bias(q + 1, i, nh)
             if live(q + 4):
                 norm_of_sp(q + 4, 1)
-            if live(q + 3):
-                row_scale(q + 3)
             if live(q + 2):
                 quantise(PAIR * (q + 2))
                 multiply(PAIR * (q + 2), 0)
                 multiply(PAIR * (q + 2), 1)
             if live(q + 1):
                 row_factors(q + 1, 0)
-                time_square(q, 0)
             if live(q + 3):
-                log_map(q + 3, 0)
-                turn(PAIR * (q + 3))
+                row_scale(q + 3)
             if live(q + 1):
                 row_factors(q + 1, 1)
-                time_square(q, 1)
-            if live(q + 3):
-                log_map(q + 3, 1)
-            if live(q + 1):
-                row_factors(q + 1, 2)
             if live(q + 2):
                 quantise(PAIR * (q + 2) + 1)
                 multiply(PAIR * (q + 2) + 1, 0)
             if live(q + 1):
+                row_factors(q + 1, 2)
+            if live(q + 3):
+                log_map(q + 3, 0)
+                turn(PAIR * (q + 3))
+            if live(q + 1):
                 row_factors(q + 1, 3)
-            if live(q - 1) and not last:
-                time_column(q - 1)
-                store(PAIR * (q - 1), PAIR * q)
+            if live(q + 3):
+                log_map(q + 3, 1)
 
         V, S = nc.vector, nc.scalar
         bias_spread()
@@ -506,7 +511,7 @@ def tile_hyperboliclinearhyperboloid_kernel(tc, x, weight, bias, out):
         arccosh_sum(0, TILES)
         arccosh_log(0, TILES)
         load_table(ACT.Exp)
-        root_of_sp(0)
+        roots(0)
         bias_root()
         bias_copy(1)
         weight_turn(0, 0, clock=True)
@@ -516,14 +521,16 @@ def tile_hyperboliclinearhyperboloid_kernel(tc, x, weight, bias, out):
         weight_regroup(0, 0, V)
         row_scale(0)
         weight_regroup(0, 1, V)
+        weight_turn(2, 0, clock=True)
         log_map(0, 0)
         turn(0)
         log_map(0, 1)
+        weight_turn(2, 1)
         weight_regroup(1, 0, V)
         regroup(0)
-        weight_turn(2, 0, clock=True)
-        weight_turn(2, 1)
+        weight_turn(3, 0, clock=True)
         turn(1)
+        weight_turn(3, 1)
         weight_regroup(1, 1, V)
         weight_quantise(0, 0)
         weight_quantise(0, 1)
@@ -531,8 +538,6 @@ def tile_hyperboliclinearhyperboloid_kernel(tc, x, weight, bias, out):
         weight_quantise(1, 1)
         quantise(0)
         multiply(0, 0)
-        weight_turn(3, 0)
-        weight_turn(3, 1)
         bias_exps()
         weight_regroup(2, 0, S)
         regroup(1)
@@ -547,7 +552,7 @@ def tile_hyperboliclinearhyperboloid_kernel(tc, x, weight, bias, out):
         weight_quantise(2, 1)
         dot_with_bias(0, 0, 0)
         norm_of_sp(1, 1)
-        root_of_sp(1)
+        roots(1)
         norm_of_h(0, 1, 0)
         weight_regroup(3, 1, V)
         weight_quantise(3, 0)
@@ -557,16 +562,16 @@ def tile_hyperboliclinearhyperboloid_kernel(tc, x, weight, bias, out):
         row_scale(1)
         dot_with_bias(0, 1, 0)
         log_map(1, 0)
-        turn(2)
+        turn(2, clock=True)
         log_map(1, 1)
         norm_of_sp(2, 0)
         norm_of_h(0, 0, 1)
         norm_of_h(0, 1, 1)
         roots_of_h(0)
-        norm_of_sp(2, 1)
-        root_of_sp(2)
         regroup(2)
         turn(3)
+        norm_of_sp(2, 1)
+        roots(2)
         bias_scaled()
         dot_with_bias(0, 0, 1)
         dot_with_bias(0, 1, 1)

@@ -197,9 +197,9 @@ def tile_hyperboliclinearhyperboloid_kernel(tc, x, weight, bias, out):
         w_grouped = {}
 
         def keep_clock(bank):
-            for nh in range(BANKS):
+            for half_bank in range(2):
                 nc.tensor.matmul(
-                    bank, lhsT=ones[:], rhs=bias_row[:, nh * BANK : (nh + 1) * BANK], start=True, stop=True
+                    bank[:, half_bank * P : (half_bank + 1) * P], lhsT=ident_f[:], rhs=ident_f[:], start=True, stop=True
                 )
 
         def weight_turn(c, g, clock=False):
@@ -306,9 +306,11 @@ def tile_hyperboliclinearhyperboloid_kernel(tc, x, weight, bias, out):
             )
             tiles[("uq", t)] = (u_codes, u_scales)
 
-        def multiply(t, nh):
+        def multiply(t, nh, clock=False):
             u_codes, u_scales = tiles[("uq", t)]
             h = psum_h.tile([P, BANK], F32, tag="h", name="h")
+            if clock:
+                keep_clock(h)
             for g in range(PASSES):
                 nc.tensor.matmul_mx(
                     out=h[:],
@@ -477,7 +479,7 @@ def tile_hyperboliclinearhyperboloid_kernel(tc, x, weight, bias, out):
                 norm_of_sp(q + 4, 1)
             if live(q + 2):
                 quantise(PAIR * (q + 2))
-                multiply(PAIR * (q + 2), 0)
+                multiply(PAIR * (q + 2), 0, clock=True)
                 multiply(PAIR * (q + 2), 1)
             if live(q + 1):
                 row_factors(q + 1, 0)
@@ -557,7 +559,7 @@ def tile_hyperboliclinearhyperboloid_kernel(tc, x, weight, bias, out):
         weight_regroup(3, 1, V)
         weight_quantise(3, 0)
         weight_quantise(3, 1)
-        multiply(0, 1)
+        multiply(0, 1, clock=True)
         multiply(1, 1)
         row_scale(1)
         dot_with_bias(0, 1, 0)

@@ -26,7 +26,6 @@ BANK = 512
 BANKS = N // BANK
 W_CHUNK = 256
 W_CHUNKS = N // W_CHUNK
-X_SLOT = 1040
 THETA_MAX = 15.0
 EXP_MAX = math.exp(THETA_MAX)
 TANH_MAX = math.tanh(0.5 * THETA_MAX)
@@ -55,11 +54,11 @@ def tile_hyperboliclinearhyperboloid_kernel(tc, x, weight, bias, out):
         x_head = keep.tile([P, TILES, 16], BF16)
         bias_row = keep.tile([P, N], BF16)
         bias_bc = keep.tile([P, N], BF16)
-        x_sb = keep.tile([P, TILES, X_SLOT], BF16)
+        x_sb = keep.tile([P, TILES, K], BF16)
         w_sb = keep.tile([P, W_CHUNKS, W_CHUNK // P, K], BF16)
 
         def load_x(t0, t1):
-            nc.sync.dma_start(out=x_sb[:, t0:t1, 1 : K + 2], in_=x_rows[:, t0:t1, :])
+            nc.sync.dma_start(out=x_sb[:, t0:t1, :], in_=x_rows[:, t0:t1, 1 : K + 1])
 
         def load_w(c):
             nc.sync.dma_start(out=w_sb[:, c, :, :], in_=w_rows[:, c, :, :])
@@ -244,7 +243,7 @@ def tile_hyperboliclinearhyperboloid_kernel(tc, x, weight, bias, out):
             return tiles[("squares", q)]
 
         def sp(t):
-            return x_sb[:, t, 2 : K + 2]
+            return x_sb[:, t, :]
 
         def norm_of_sp(q, i, on_vector=False):
             junk_a = junk.tile([P, K], F32, tag="junk_a", name="junk_a")

@@ -30,6 +30,7 @@ THETA_MAX = 15.0
 EXP_MAX = math.exp(THETA_MAX)
 TANH_MAX = math.tanh(0.5 * THETA_MAX)
 BEHIND = 3
+SLOW_COLS = 256
 ALIGN = 8
 
 FLOPS = 2 * ROWS * K * N
@@ -413,6 +414,32 @@ def tile_hyperboliclinearhyperboloid_kernel(tc, x, weight, bias, out):
                 op0=ALU.mult, op1=ALU.add,
             )
 
+        def split_column(q):
+            c0 = OUT_W * (PAIR * q + 1) + 1 + BANK
+            return c0, (c0 + BANK - SLOW_COLS + ALIGN - 1) // ALIGN * ALIGN, c0 + BANK
+
+        def scaled_part(q):
+            c0, c1, c2 = split_column(q)
+            part = junk.tile([P, BANK], F32, name="part")
+            nc.scalar.activation(
+                out=part[:, 0 : c2 - c1], in_=tiles[("h", PAIR * q + 1, BANKS - 1)][:, c1 - c0 : BANK],
+                func=ACT.Identity, scale=tiles[("va", q)][:, 5, 1:2],
+            )
+            tiles[("part", q)] = part
+
+        def finish_part(q):
+            c0, c1, c2 = split_column(q)
+            nc.gpsimd.tensor_tensor(
+                out=o_all[:, c1:c2], in0=tiles[("part", q)][:, 0 : c2 - c1], in1=bias_s[:, N - (c2 - c1) : N], op=ALU.add
+            )
+
+        def finish_rest(q):
+            c0, c1, c2 = split_column(q)
+            nc.vector.scalar_tensor_tensor(
+                out=o_all[:, c0:c1], in0=tiles[("h", PAIR * q + 1, BANKS - 1)][:, 0 : c1 - c0],
+                scalar=tiles[("va", q)][:, 5, 1:2], in1=bias_s[:, BANK : BANK + c1 - c0], op0=ALU.mult, op1=ALU.add,
+            )
+
         def time_column(q):
             c0 = OUT_W * PAIR * q
             for i in range(PAIR):
@@ -430,6 +457,10 @@ def tile_hyperboliclinearhyperboloid_kernel(tc, x, weight, bias, out):
             if live(q + 1):
                 norm_of_h(q + 1, 0, 0)
                 norm_of_h(q + 1, 0, 1)
+            if not last:
+                scaled_part(q)
+                finish_part(q)
+            if live(q + 1):
                 norm_of_h(q + 1, 1, 0)
             if last:
                 time_square(q, 0)
@@ -459,7 +490,10 @@ def tile_hyperboliclinearhyperboloid_kernel(tc, x, weight, bias, out):
             finish(q, 1, 0)
             if last:
                 store(c0 + OUT_W, c0 + OUT_W + 1 + BANK)
-            finish(q, 1, 1)
+            if last:
+                finish(q, 1, 1)
+            else:
+                finish_rest(q)
             if last:
                 store(c0 + OUT_W + 1 + BANK, c0 + PAIR * OUT_W)
             if live(q + 4):

@@ -332,12 +332,16 @@ def tile_hyperboliclinearhyperboloid_kernel(tc, x, weight, bias, out):
                 accum_out=tiles[("hh2", q)][:, i, nh : nh + 1],
             )
 
-        def roots_of_h(q):
-            hg = small.tile([P, 2, PAIR], F32, name="hg")
+        def pair_tile(name, q, parts):
+            if (name, q) not in tiles:
+                tiles[(name, q)] = small.tile([P, parts, PAIR], F32, name=name)
+            return tiles[(name, q)]
+
+        def roots_of_h(q, i0=0, i1=PAIR):
+            hg = pair_tile("hg", q, 2)
             hh2 = tiles[("hh2", q)]
-            nc.gpsimd.tensor_tensor(out=hg[:, 0, :], in0=hh2[:, :, 0], in1=hh2[:, :, 1], op=ALU.add)
-            nc.gpsimd.tensor_tensor(out=hg[:, 1, :], in0=hg[:, 0, :], in1=half[:, 0:PAIR], op=ALU.pow)
-            tiles[("hg", q)] = hg
+            nc.gpsimd.tensor_tensor(out=hg[:, 0, i0:i1], in0=hh2[:, i0:i1, 0], in1=hh2[:, i0:i1, 1], op=ALU.add)
+            nc.gpsimd.tensor_tensor(out=hg[:, 1, i0:i1], in0=hg[:, 0, i0:i1], in1=half[:, i0:i1], op=ALU.pow)
 
         def dot_with_bias(q, i, nh):
             if i == 0 and nh == 0:
@@ -349,24 +353,21 @@ def tile_hyperboliclinearhyperboloid_kernel(tc, x, weight, bias, out):
                 op0=ALU.mult, op1=ALU.mult, accum_out=tiles[("hb", q)][:, i, nh : nh + 1],
             )
 
-        def exponentials(q):
-            norm = tiles[("hg", q)][:, 1, :]
-            ex = small.tile([P, 3, PAIR], F32, name="ex")
-            nc.scalar.activation(out=ex[:, 0, :], in_=norm, func=ACT.Exp)
-            nc.scalar.activation(out=ex[:, 1, :], in_=norm, func=ACT.Exp, scale=-1.0)
-            nc.scalar.activation(out=ex[:, 2, :], in_=norm, func=ACT.Tanh, scale=0.5)
-            tiles[("ex", q)] = ex
+        def exponentials(q, i0=0, i1=PAIR):
+            norm = tiles[("hg", q)][:, 1, i0:i1]
+            ex = pair_tile("ex", q, 3)
+            nc.scalar.activation(out=ex[:, 0, i0:i1], in_=norm, func=ACT.Exp)
+            nc.scalar.activation(out=ex[:, 1, i0:i1], in_=norm, func=ACT.Exp, scale=-1.0)
+            nc.scalar.activation(out=ex[:, 2, i0:i1], in_=norm, func=ACT.Tanh, scale=0.5)
 
-        def row_factors(q, step):
-            ex = tiles[("ex", q)]
+        def row_factors(q, step, i0=0, i1=PAIR):
             hb = tiles[("hb", q)]
-            if step == 0:
-                tiles[("va", q)] = small.tile([P, 7, PAIR], F32, name="va")
-            va = tiles[("va", q)]
+            ex = tiles[("ex", q)][:, :, i0:i1]
+            va = pair_tile("va", q, 7)[:, :, i0:i1]
             r_inv = va[:, 6, :]
             if step == 0:
-                nc.vector.reciprocal(out=r_inv, in_=tiles[("hg", q)][:, 1, :])
-                nc.vector.tensor_tensor(out=va[:, 0, :], in0=hb[:, :, 0], in1=hb[:, :, 1], op=ALU.add)
+                nc.vector.reciprocal(out=r_inv, in_=tiles[("hg", q)][:, 1, i0:i1])
+                nc.vector.tensor_tensor(out=va[:, 0, :], in0=hb[:, i0:i1, 0], in1=hb[:, i0:i1, 1], op=ALU.add)
                 nc.vector.scalar_tensor_tensor(
                     out=va[:, 1, :], in0=ex[:, 0, :], scalar=EXP_MAX, in1=ex[:, 1, :], op0=ALU.min, op1=ALU.subtract
                 )
@@ -386,24 +387,29 @@ def tile_hyperboliclinearhyperboloid_kernel(tc, x, weight, bias, out):
                     out=va[:, 5, :], in0=va[:, 4, :], scalar=cosh_half, in1=va[:, 3, :], op0=ALU.add, op1=ALU.mult
                 )
 
-        def time_square(q, step):
-            va = tiles[("va", q)]
+        def time_square(q, step, i0=0, i1=PAIR):
+            va = tiles[("va", q)][:, :, i0:i1]
+            vt = pair_tile("vt", q, 2)[:, :, i0:i1]
             if step == 0:
-                tiles[("vt", q)] = small.tile([P, 2, PAIR], F32, name="vt")
-            vt = tiles[("vt", q)]
-            if step == 0:
-                nc.vector.tensor_tensor(out=vt[:, 0, :], in0=va[:, 5, :], in1=tiles[("hg", q)][:, 0, :], op=ALU.mult)
+                hh = tiles[("hg", q)][:, 0, i0:i1]
+                nc.vector.tensor_tensor(out=vt[:, 0, :], in0=va[:, 5, :], in1=hh, op=ALU.mult)
             elif step == 1:
                 nc.vector.scalar_tensor_tensor(
                     out=vt[:, 1, :], in0=va[:, 0, :], scalar=4.0, in1=vt[:, 0, :], op0=ALU.mult, op1=ALU.add
                 )
             else:
-                for i in range(PAIR):
+                for i in range(i1 - i0):
                     nc.scalar.activation(
-                        out=squares_of(q + BEHIND)[:, 0, i : i + 1], in_=vt[:, 1, i : i + 1], func=ACT.Identity,
-                        scale=va[:, 5, i : i + 1], bias=one_plus,
+                        out=squares_of(q + BEHIND)[:, 0, i0 + i : i0 + i + 1], in_=vt[:, 1, i : i + 1],
+                        func=ACT.Identity, scale=va[:, 5, i : i + 1], bias=one_plus,
                     )
 
+        def time_root(q, i):
+            both = pair_tile("alone", q, 2)
+            tiles[("roots", q + BEHIND)] = both
+            nc.gpsimd.tensor_tensor(
+                out=both[:, 0, i : i + 1], in0=squares_of(q + BEHIND)[:, 0, i : i + 1], in1=half[:, i : i + 1], op=ALU.pow
+            )
 
         def finish(q, i, nh):
             t = PAIR * q + i
@@ -440,9 +446,9 @@ def tile_hyperboliclinearhyperboloid_kernel(tc, x, weight, bias, out):
                 scalar=tiles[("va", q)][:, 5, 1:2], in1=bias_s[:, BANK : BANK + c1 - c0], op0=ALU.mult, op1=ALU.add,
             )
 
-        def time_column(q):
+        def time_column(q, i0=0, i1=PAIR):
             c0 = OUT_W * PAIR * q
-            for i in range(PAIR):
+            for i in range(i0, i1):
                 nc.scalar.copy(
                     out=o_all[:, c0 + i * OUT_W : c0 + i * OUT_W + 1], in_=tiles[("roots", q + BEHIND)][:, 0, i : i + 1]
                 )
@@ -451,85 +457,103 @@ def tile_hyperboliclinearhyperboloid_kernel(tc, x, weight, bias, out):
             cols = slice(c0 // ALIGN * ALIGN, c1 // ALIGN * ALIGN)
             nc.sync.dma_start(out=out_flat[:, cols], in_=o_all[:, cols])
 
-        def period(q):
-            last = q == PAIRS - 1
+        def last_pair(q):
             c0 = OUT_W * PAIR * q
-            if live(q + 1):
-                norm_of_h(q + 1, 0, 0)
-                norm_of_h(q + 1, 0, 1)
-            if not last:
-                scaled_part(q)
-                finish_part(q)
-            if live(q + 1):
-                norm_of_h(q + 1, 1, 0)
-            if last:
-                time_square(q, 0)
-                time_square(q, 1)
-                time_square(q, 2)
-                roots(q + BEHIND)
-                time_column(q)
+            a, b = c0 + ALIGN, c0 + OUT_W + ALIGN
+            dot_with_bias(q, 0, 0)
+            dot_with_bias(q, 0, 1)
+            dot_with_bias(q, 1, 0)
+            row_factors(q, 0, 0, 1)
+            row_factors(q, 1, 0, 1)
+            dot_with_bias(q, 1, 1)
+            row_factors(q, 2, 0, 1)
+            row_factors(q, 0, 1, 2)
+            row_factors(q, 3, 0, 1)
+            row_factors(q, 1, 1, 2)
+            time_square(q, 0, 0, 1)
             finish(q, 0, 0)
-            if live(q + 1):
-                multiply(PAIR * (q + 1) + 1, 1)
-            if not last:
-                time_square(q, 0)
+            time_square(q, 1, 0, 1)
+            time_square(q, 2, 0, 1)
+            time_root(q, 0)
+            time_column(q, 0, 1)
+            row_factors(q, 2, 1, 2)
             finish(q, 0, 1)
-            if not last:
-                time_square(q, 1)
-                time_square(q, 2)
-                roots(q + BEHIND)
+            store(a, c0 + OUT_W)
+            row_factors(q, 3, 1, 2)
+            time_square(q, 0, 1, 2)
+            finish(q, 1, 0)
+            store(b, c0 + OUT_W + 1 + BANK)
+            time_square(q, 1, 1, 2)
+            time_square(q, 2, 1, 2)
+            time_root(q, 1)
+            time_column(q, 1, 2)
+            finish(q, 1, 1)
+            store(c0 + OUT_W + 1 + BANK, c0 + PAIR * OUT_W)
+            store(c0, a)
+            store(c0 + OUT_W, b)
+
+        def period(q):
+            last = q + 1 == PAIRS - 1
+            c0 = OUT_W * PAIR * q
+            norm_of_h(q + 1, 0, 0)
+            norm_of_h(q + 1, 0, 1)
+            if last:
+                roots_of_h(q + 1, 0, 1)
+            scaled_part(q)
+            finish_part(q)
+            norm_of_h(q + 1, 1, 0)
+            finish(q, 0, 0)
+            multiply(PAIR * (q + 1) + 1, 1)
+            time_square(q, 0)
+            finish(q, 0, 1)
+            time_square(q, 1)
+            time_square(q, 2)
+            roots(q + BEHIND)
+            if last:
+                exponentials(q + 1, 0, 1)
             if live(q + 2):
                 regroup(PAIR * (q + 2))
-            if live(q + 1):
-                norm_of_h(q + 1, 1, 1)
+            norm_of_h(q + 1, 1, 1)
+            if last:
+                roots_of_h(q + 1, 1, 2)
+            else:
                 roots_of_h(q + 1)
             if live(q + 2):
                 turn(PAIR * (q + 2) + 1, clock=True)
-            if last:
-                store(c0, c0 + OUT_W)
             finish(q, 1, 0)
-            if last:
-                store(c0 + OUT_W, c0 + OUT_W + 1 + BANK)
-            if last:
-                finish(q, 1, 1)
-            else:
-                finish_rest(q)
-            if last:
-                store(c0 + OUT_W + 1 + BANK, c0 + PAIR * OUT_W)
+            finish_rest(q)
             if live(q + 4):
                 norm_of_sp(q + 4, 0)
-            if not last:
-                time_column(q)
-                store(c0, c0 + PAIR * OUT_W)
+            time_column(q)
+            store(c0, c0 + PAIR * OUT_W)
             if live(q + 2):
                 regroup(PAIR * (q + 2) + 1)
-            if live(q + 1):
-                exponentials(q + 1)
-                for i in range(PAIR):
-                    for nh in range(BANKS):
-                        dot_with_bias(q + 1, i, nh)
+            if last:
+                exponentials(q + 1, 1, 2)
+                last_pair(q + 1)
+                return
+            exponentials(q + 1)
+            for i in range(PAIR):
+                for nh in range(BANKS):
+                    dot_with_bias(q + 1, i, nh)
             if live(q + 4):
                 norm_of_sp(q + 4, 1)
             if live(q + 2):
                 quantise(PAIR * (q + 2))
                 multiply(PAIR * (q + 2), 0, clock=True)
                 multiply(PAIR * (q + 2), 1)
-            if live(q + 1):
-                row_factors(q + 1, 0)
+            row_factors(q + 1, 0)
             if live(q + 3):
                 row_scale(q + 3)
-            if live(q + 1):
-                row_factors(q + 1, 1)
+            row_factors(q + 1, 1)
             if live(q + 2):
                 quantise(PAIR * (q + 2) + 1)
                 multiply(PAIR * (q + 2) + 1, 0)
-            if live(q + 1):
-                row_factors(q + 1, 2)
+            row_factors(q + 1, 2)
             if live(q + 3):
                 log_map(q + 3, 0)
                 turn(PAIR * (q + 3))
-            if live(q + 1):
-                row_factors(q + 1, 3)
+            row_factors(q + 1, 3)
             if live(q + 3):
                 log_map(q + 3, 1)
 
@@ -627,5 +651,5 @@ def tile_hyperboliclinearhyperboloid_kernel(tc, x, weight, bias, out):
         log_map(2, 1)
         norm_of_sp(3, 0)
         norm_of_sp(3, 1)
-        for q in range(PAIRS):
+        for q in range(PAIRS - 1):
             period(q)

import math
from contextlib import ExitStack

import concourse.mybir as mybir
from concourse.masks import make_identity

FP8X4 = mybir.dt.float8_e4m3fn_x4
BF16 = mybir.dt.bfloat16
F32 = mybir.dt.float32
U32 = mybir.dt.uint32
U8 = mybir.dt.uint8
ALU = mybir.AluOpType
ACT = mybir.ActivationFunctionType

P = 128
ROWS = 2048
K = 1024
N = 1024
OUT_W = N + 1
TILES = ROWS // P
PAIR = 2
PAIRS = TILES // PAIR
K_PASS = 512
PASSES = K // K_PASS
BANK = 512
BANKS = N // BANK
W_CHUNK = 256
W_CHUNKS = N // W_CHUNK
THETA_MAX = 15.0
EXP_MAX = math.exp(THETA_MAX)
TANH_MAX = math.tanh(0.5 * THETA_MAX)
BEHIND = 3
SLOW_COLS = 256
ALIGN = 8

FLOPS = 2 * ROWS * K * N


def tile_hyperboliclinearhyperboloid_kernel(tc, x, weight, bias, out):
    nc = tc.nc
    with ExitStack() as stack:
        keep = stack.enter_context(tc.tile_pool(name="keep", bufs=1))
        wstage = stack.enter_context(tc.tile_pool(name="wstage", bufs=4))
        upool = stack.enter_context(tc.tile_pool(name="upool", bufs=4))
        junk = stack.enter_context(tc.tile_pool(name="junk", bufs=3))
        small = stack.enter_context(tc.tile_pool(name="small", bufs=4))
        psum_t = stack.enter_context(tc.psum_pool(name="psum_t", bufs=1))
        psum_h = stack.enter_context(tc.psum_pool(name="psum_h", bufs=7))
        stack.enter_context(tc.manual_schedule())

        x_rows = x.rearrange("(p t) c -> p t c", t=TILES)
        out_flat = out.rearrange("(p t) c -> p (t c)", t=TILES)
        w_rows = weight.rearrange("(c b p) k -> p c b k", b=W_CHUNK // P, p=P)

        x_head = keep.tile([P, TILES, 16], BF16)
        bias_row = keep.tile([P, N], BF16)
        bias_bc = keep.tile([P, N], BF16)
        x_sb = keep.tile([P, TILES, K], BF16)
        w_sb = keep.tile([P, W_CHUNKS, W_CHUNK // P, K], BF16)

        def load_x(t0, t1):
            nc.sync.dma_start(out=x_sb[:, t0:t1, :], in_=x_rows[:, t0:t1, 1 : K + 1])

        def load_w(c):
            nc.sync.dma_start(out=w_sb[:, c, :, :], in_=w_rows[:, c, :, :])

        nc.gpsimd.memset(bias_row[:].bitcast(F32), 0.0)
        nc.scalar.dma_start(out=x_head[:], in_=x_rows[:, :, 0:16])
        nc.sync.dma_start(out=bias_row[0:1, :], in_=bias)
        load_x(0, 1)
        load_x(1, 2)
        load_w(0)
        load_w(1)
        load_w(2)
        load_w(3)
        load_x(2, 4)
        load_x(4, 6)
        load_x(6, 8)
        load_x(8, 12)
        load_x(12, 16)

        ident_f = keep.tile([P, P], F32)
        make_identity(nc, ident_f[:])
        minus_half = keep.tile([P, PAIR], F32)
        nc.vector.memset(minus_half[:], -0.5)
        half = keep.tile([P, TILES], F32)
        nc.vector.memset(half[:], 0.5)
        powers = keep.tile([P, 2, PAIR], F32)
        nc.vector.memset(powers[:, 0, :], 0.5)
        nc.vector.memset(powers[:, 1, :], -0.5)
        ones = keep.tile([P, P], BF16)
        nc.gpsimd.memset(ones[:], 1.0)
        warm = keep.tile([P, 1], F32)
        nc.scalar.activation(out=warm[:], in_=half[:, 0:1], func=ACT.Sqrt)

        tiles = {}

        dist = keep.tile([P, TILES], F32)

        def arccosh_square(times, t0, t1):
            n = t1 - t0
            theta0 = small.tile([P, TILES], F32, name="theta0")
            nc.vector.tensor_scalar(out=theta0[:, 0:n], in0=times, scalar1=1.0 + 1e-7, scalar2=None, op0=ALU.max)
            theta0_m1 = small.tile([P, TILES], F32, name="theta0_m1")
            nc.vector.tensor_scalar(out=theta0_m1[:, 0:n], in0=theta0[:, 0:n], scalar1=-1.0, scalar2=None, op0=ALU.add)
            theta0_sq = small.tile([P, TILES], F32, name="theta0_sq")
            nc.vector.scalar_tensor_tensor(
                out=theta0_sq[:, 0:n], in0=theta0[:, 0:n], scalar=1.0, in1=theta0_m1[:, 0:n],
                op0=ALU.add, op1=ALU.mult,
            )
            tiles[("theta0", t0)] = (theta0, theta0_sq)

        def arccosh_root(t0, t1):
            n = t1 - t0
            theta0, theta0_sq = tiles[("theta0", t0)]
            theta0_rt = small.tile([P, TILES], F32, name="theta0_rt")
            nc.scalar.activation(out=theta0_rt[:, 0:n], in_=theta0_sq[:, 0:n], func=ACT.Sqrt)
            tiles[("theta0", t0)] = (theta0, theta0_rt)

        def arccosh_sum(t0, t1):
            n = t1 - t0
            theta0, theta0_rt = tiles[("theta0", t0)]
            theta0_sum = small.tile([P, TILES], F32, name="theta0_sum")
            nc.vector.tensor_tensor(out=theta0_sum[:, 0:n], in0=theta0[:, 0:n], in1=theta0_rt[:, 0:n], op=ALU.add)
            tiles[("theta0", t0)] = theta0_sum

        def arccosh_log(t0, t1):
            nc.scalar.activation(out=dist[:, t0:t1], in_=tiles[("theta0", t0)][:, 0 : t1 - t0], func=ACT.Ln)

        bb2 = keep.tile([P, BANKS], F32)
        bb = keep.tile([P, 1], F32)
        t_g = keep.tile([P, 3], F32)
        t_b = t_g[:, 2:3]
        t_e = keep.tile([P, 2], F32)
        t_v = keep.tile([P, 6], F32)
        t_inv = t_v[:, 0:1]
        cosh_half = t_v[:, 1:2]
        sinc2 = t_v[:, 2:3]
        sinc_half = t_v[:, 5:6]
        one_plus = t_v[:, 4:5]
        bias_s = keep.tile([P, N], F32)

        def bias_spread():
            spread = []
            for nh in range(BANKS):
                bank = psum_h.tile([P, BANK], F32, tag="h", name="bank")
                nc.tensor.matmul(
                    bank[:], lhsT=ones[:], rhs=bias_row[:, nh * BANK : (nh + 1) * BANK], start=True, stop=True
                )
                spread.append(bank)
            tiles["spread"] = spread

        def bias_copy(nh):
            nc.vector.tensor_copy(out=bias_bc[:, nh * BANK : (nh + 1) * BANK], in_=tiles["spread"][nh][:])

        def bias_square(nh):
            junk_b = junk.tile([P, BANK], F32, tag="junk_s", name="junk_b")
            nc.scalar.activation(
                out=junk_b[:], in_=tiles["spread"][nh][:], func=ACT.Square, accum_out=bb2[:, nh : nh + 1]
            )

        def bias_root():
            nc.gpsimd.tensor_tensor(out=bb[:], in0=bb2[:, 0:1], in1=bb2[:, 1:2], op=ALU.add)
            nc.gpsimd.tensor_scalar(out=t_g[:, 0:1], in0=bb[:], scalar1=1e-15, scalar2=None, op0=ALU.max)
            nc.gpsimd.tensor_tensor(out=t_g[:, 1:2], in0=t_g[:, 0:1], in1=half[:, 0:1], op=ALU.pow)
            nc.gpsimd.tensor_scalar(out=t_b, in0=t_g[:, 1:2], scalar1=1e-15, scalar2=15.0, op0=ALU.max, op1=ALU.min)

        def load_table(func):
            nc.scalar.activation(out=warm[:], in_=half[:, 0:1], func=func)

        def bias_exps():
            nc.scalar.activation(out=t_e[:, 0:1], in_=t_b, func=ACT.Exp)
            nc.scalar.activation(out=t_e[:, 1:2], in_=t_b, func=ACT.Exp, scale=-1.0)

        def bias_factors():
            nc.vector.reciprocal(out=t_inv, in_=t_b)
            nc.vector.tensor_scalar(
                out=cosh_half, in0=t_e[:, 0:1], scalar1=t_e[:, 1:2], scalar2=0.25, op0=ALU.add, op1=ALU.mult
            )
            nc.vector.scalar_tensor_tensor(
                out=sinc2, in0=t_e[:, 0:1], scalar=t_e[:, 1:2], in1=t_inv, op0=ALU.subtract, op1=ALU.mult
            )
            nc.vector.tensor_scalar(out=sinc_half, in0=sinc2, scalar1=0.25, scalar2=None, op0=ALU.mult)
            nc.vector.scalar_tensor_tensor(
                out=t_v[:, 3:4], in0=sinc2, scalar=sinc2, in1=bb[:], op0=ALU.mult, op1=ALU.mult
            )
            nc.vector.tensor_scalar(out=one_plus, in0=t_v[:, 3:4], scalar1=0.25, scalar2=1.0, op0=ALU.mult, op1=ALU.add)

        def bias_scaled():
            nc.vector.tensor_scalar(
                out=bias_s[:], in0=bias_bc[:], scalar1=sinc2, scalar2=0.5, op0=ALU.mult, op1=ALU.mult
            )

        w_codes = keep.tile([P, PASSES, N], U32, align_bytes=64)
        w_scales = keep.tile([P, PASSES, N], U8, align_bytes=64)
        w_words = w_sb[:].bitcast(F32)
        w_grouped = {}

        def keep_clock(bank):
            for half_bank in range(2):
                nc.tensor.matmul(
                    bank[:, half_bank * P : (half_bank + 1) * P], lhsT=ident_f[:], rhs=ident_f[:], start=True, stop=True
                )

        def weight_turn(c, g, clock=False):
            wt = psum_h.tile([P, 2, W_CHUNK], F32, tag="h", name="wt")
            if clock:
                keep_clock(wt[:].rearrange("p u n -> p (u n)"))
            for u in range(2):
                for b in range(W_CHUNK // P):
                    nc.tensor.transpose(
                        wt[:, u, b * P : (b + 1) * P],
                        w_words[:, c, b, 256 * g + u : 256 * (g + 1) : 2],
                        ident_f[:],
                    )
            tiles[("wt", c, g)] = wt

        def weight_regroup(c, g, engine):
            grouped = wstage.tile([P, W_CHUNK, 4], BF16, align_bytes=64, name="grouped")
            out_words = grouped[:].bitcast(F32)
            in_words = tiles[("wt", c, g)][:].rearrange("p u n -> p n u")
            if engine is nc.vector:
                nc.vector.tensor_copy(out=out_words, in_=in_words)
            else:
                nc.scalar.copy(out=out_words, in_=in_words)
            w_grouped[(c, g)] = grouped

        def weight_quantise(c, g):
            n_cols = slice(c * W_CHUNK, (c + 1) * W_CHUNK)
            nc.vector.quantize_mx(
                out=w_codes[:, g, n_cols].bitcast(FP8X4),
                scales=w_scales[:, g, n_cols],
                in_=w_grouped[(c, g)][:].rearrange("p n j -> p (n j)"),
            )

        o_all = keep.tile([P, TILES * OUT_W], F32)

        def live(q):
            return 0 <= q < PAIRS

        def squares_of(q):
            if ("squares", q) not in tiles:
                tiles[("squares", q)] = small.tile([P, 2, PAIR], F32, name="squares")
            return tiles[("squares", q)]

        def sp(t):
            return x_sb[:, t, :]

        def norm_of_sp(q, i, on_vector=False):
            junk_a = junk.tile([P, K], F32, tag="junk_a", name="junk_a")
            total = squares_of(q)[:, 1, i : i + 1]
            if on_vector:
                nc.vector.scalar_tensor_tensor(
                    out=junk_a[:], in0=sp(PAIR * q + i), scalar=1.0, in1=sp(PAIR * q + i),
                    op0=ALU.mult, op1=ALU.mult, accum_out=total,
                )
            else:
                nc.scalar.activation(out=junk_a[:], in_=sp(PAIR * q + i), func=ACT.Square, accum_out=total)

        def roots(q):
            which = slice(0 if live(q - BEHIND) else 1, 2 if live(q) else 1)
            both = small.tile([P, 2, PAIR], F32, name="both")
            nc.gpsimd.tensor_tensor(
                out=both[:, which, :], in0=squares_of(q)[:, which, :], in1=powers[:, which, :], op=ALU.pow
            )
            tiles[("roots", q)] = both

        def row_scale(q):
            s_row = small.tile([P, PAIR], F32, name="s_row")
            nc.vector.scalar_tensor_tensor(
                out=s_row[:], in0=tiles[("roots", q)][:, 1, :], scalar=1e15, in1=dist[:, PAIR * q : PAIR * (q + 1)],
                op0=ALU.min, op1=ALU.mult,
            )
            tiles[("s", q)] = s_row

        def log_map(q, i):
            t = PAIR * q + i
            u_bf = upool.tile([P, K], BF16, name="u_bf")
            nc.vector.tensor_scalar(
                out=u_bf[:], in0=sp(t), scalar1=tiles[("s", q)][:, i : i + 1], scalar2=None, op0=ALU.mult
            )
            tiles[("u", t)] = u_bf

        def turn(t, clock=False):
            ut = psum_t.tile([P, PASSES, 2, P], F32, name="ut")
            if clock:
                keep_clock(ut[:].rearrange("p g u m -> p (g u m)"))
            u_words = tiles[("u", t)][:].bitcast(F32)
            for g in range(PASSES):
                for u in range(2):
                    nc.tensor.transpose(ut[:, g, u, :], u_words[:, 256 * g + u : 256 * (g + 1) : 2], ident_f[:])
            tiles[("ut", t)] = ut

        def regroup(t):
            u_grouped = upool.tile([P, PASSES, P, 4], BF16, align_bytes=64, name="u_grouped")
            nc.scalar.copy(out=u_grouped[:].bitcast(F32), in_=tiles[("ut", t)][:].rearrange("p g u m -> p g m u"))
            tiles[("ug", t)] = u_grouped

        def quantise(t):
            u_codes = upool.tile([P, PASSES * P], U32, align_bytes=64, name="u_codes")
            u_scales = upool.tile([P, PASSES * P], U8, align_bytes=64, name="u_scales")
            nc.vector.quantize_mx(
                out=u_codes[:].bitcast(FP8X4),
                scales=u_scales[:],
                in_=tiles[("ug", t)][:].rearrange("p g m j -> p (g m j)"),
            )
            tiles[("uq", t)] = (u_codes, u_scales)

        def multiply(t, nh, clock=False):
            u_codes, u_scales = tiles[("uq", t)]
            h = psum_h.tile([P, BANK], F32, tag="h", name="h")
            if clock:
                keep_clock(h)
            for g in range(PASSES):
                nc.tensor.matmul_mx(
                    out=h[:],
                    lhsT=u_codes[:, g * P : (g + 1) * P].bitcast(FP8X4),
                    lhsT_scale=u_scales[:, g * P : (g + 1) * P],
                    rhs=w_codes[:, g, nh * BANK : (nh + 1) * BANK].bitcast(FP8X4),
                    rhs_scale=w_scales[:, g, nh * BANK : (nh + 1) * BANK],
                    start=(g == 0),
                    stop=(g == PASSES - 1),
                )
            tiles[("h", t, nh)] = h

        def norm_of_h(q, i, nh):
            if i == 0 and nh == 0:
                tiles[("hh2", q)] = small.tile([P, PAIR, BANKS], F32, name="hh2")
            junk_s = junk.tile([P, BANK], F32, name="junk_s")
            nc.scalar.activation(
                out=junk_s[:], in_=tiles[("h", PAIR * q + i, nh)][:], func=ACT.Square,
                accum_out=tiles[("hh2", q)][:, i, nh : nh + 1],
            )

        def pair_tile(name, q, parts):
            if (name, q) not in tiles:
                tiles[(name, q)] = small.tile([P, parts, PAIR], F32, name=name)
            return tiles[(name, q)]

        def roots_of_h(q, i0=0, i1=PAIR):
            hg = pair_tile("hg", q, 2)
            hh2 = tiles[("hh2", q)]
            nc.gpsimd.tensor_tensor(out=hg[:, 0, i0:i1], in0=hh2[:, i0:i1, 0], in1=hh2[:, i0:i1, 1], op=ALU.add)
            nc.gpsimd.tensor_tensor(out=hg[:, 1, i0:i1], in0=hg[:, 0, i0:i1], in1=half[:, i0:i1], op=ALU.pow)

        def dot_with_bias(q, i, nh):
            if i == 0 and nh == 0:
                tiles[("hb", q)] = small.tile([P, PAIR, BANKS], F32, name="hb")
            junk_v = junk.tile([P, BANK], F32, name="junk_v")
            nc.vector.scalar_tensor_tensor(
                out=junk_v[:], in0=tiles[("h", PAIR * q + i, nh)][:], scalar=sinc_half,
                in1=bias_bc[:, nh * BANK : (nh + 1) * BANK],
                op0=ALU.mult, op1=ALU.mult, accum_out=tiles[("hb", q)][:, i, nh : nh + 1],
            )

        def exponentials(q, i0=0, i1=PAIR):
            norm = tiles[("hg", q)][:, 1, i0:i1]
            ex = pair_tile("ex", q, 3)
            nc.scalar.activation(out=ex[:, 0, i0:i1], in_=norm, func=ACT.Exp)
            nc.scalar.activation(out=ex[:, 1, i0:i1], in_=norm, func=ACT.Exp, scale=-1.0)
            nc.scalar.activation(out=ex[:, 2, i0:i1], in_=norm, func=ACT.Tanh, scale=0.5)

        def row_factors(q, step, i0=0, i1=PAIR):
            hb = tiles[("hb", q)]
            ex = tiles[("ex", q)][:, :, i0:i1]
            va = pair_tile("va", q, 7)[:, :, i0:i1]
            r_inv = va[:, 6, :]
            if step == 0:
                nc.vector.reciprocal(out=r_inv, in_=tiles[("hg", q)][:, 1, i0:i1])
                nc.vector.tensor_tensor(out=va[:, 0, :], in0=hb[:, i0:i1, 0], in1=hb[:, i0:i1, 1], op=ALU.add)
                nc.vector.scalar_tensor_tensor(
                    out=va[:, 1, :], in0=ex[:, 0, :], scalar=EXP_MAX, in1=ex[:, 1, :], op0=ALU.min, op1=ALU.subtract
                )
            elif step == 1:
                nc.vector.scalar_tensor_tensor(
                    out=va[:, 2, :], in0=ex[:, 2, :], scalar=TANH_MAX, in1=va[:, 0, :], op0=ALU.min, op1=ALU.mult
                )
                nc.vector.scalar_tensor_tensor(
                    out=va[:, 3, :], in0=r_inv, scalar=1e15, in1=va[:, 1, :], op0=ALU.min, op1=ALU.mult
                )
            elif step == 2:
                nc.vector.scalar_tensor_tensor(
                    out=va[:, 4, :], in0=r_inv, scalar=1e15, in1=va[:, 2, :], op0=ALU.min, op1=ALU.mult
                )
            else:
                nc.vector.scalar_tensor_tensor(
                    out=va[:, 5, :], in0=va[:, 4, :], scalar=cosh_half, in1=va[:, 3, :], op0=ALU.add, op1=ALU.mult
                )

        def time_square(q, step, i0=0, i1=PAIR):
            va = tiles[("va", q)][:, :, i0:i1]
            vt = pair_tile("vt", q, 2)[:, :, i0:i1]
            if step == 0:
                hh = tiles[("hg", q)][:, 0, i0:i1]
                nc.vector.tensor_tensor(out=vt[:, 0, :], in0=va[:, 5, :], in1=hh, op=ALU.mult)
            elif step == 1:
                nc.vector.scalar_tensor_tensor(
                    out=vt[:, 1, :], in0=va[:, 0, :], scalar=4.0, in1=vt[:, 0, :], op0=ALU.mult, op1=ALU.add
                )
            else:
                for i in range(i1 - i0):
                    nc.scalar.activation(
                        out=squares_of(q + BEHIND)[:, 0, i0 + i : i0 + i + 1], in_=vt[:, 1, i : i + 1],
                        func=ACT.Identity, scale=va[:, 5, i : i + 1], bias=one_plus,
                    )

        def time_root(q, i):
            both = pair_tile("alone", q, 2)
            tiles[("roots", q + BEHIND)] = both
            nc.gpsimd.tensor_tensor(
                out=both[:, 0, i : i + 1], in0=squares_of(q + BEHIND)[:, 0, i : i + 1], in1=half[:, i : i + 1], op=ALU.pow
            )

        def finish(q, i, nh):
            t = PAIR * q + i
            c0 = OUT_W * t + 1 + nh * BANK
            nc.vector.scalar_tensor_tensor(
                out=o_all[:, c0 : c0 + BANK], in0=tiles[("h", t, nh)][:],
                scalar=tiles[("va", q)][:, 5, i : i + 1], in1=bias_s[:, nh * BANK : (nh + 1) * BANK],
                op0=ALU.mult, op1=ALU.add,
            )

        def split_column(q):
            c0 = OUT_W * (PAIR * q + 1) + 1 + BANK
            return c0, (c0 + BANK - SLOW_COLS + ALIGN - 1) // ALIGN * ALIGN, c0 + BANK

        def scaled_part(q):
            c0, c1, c2 = split_column(q)
            part = junk.tile([P, BANK], F32, name="part")
            nc.scalar.activation(
                out=part[:, 0 : c2 - c1], in_=tiles[("h", PAIR * q + 1, BANKS - 1)][:, c1 - c0 : BANK],
                func=ACT.Identity, scale=tiles[("va", q)][:, 5, 1:2],
            )
            tiles[("part", q)] = part

        def finish_part(q):
            c0, c1, c2 = split_column(q)
            nc.gpsimd.tensor_tensor(
                out=o_all[:, c1:c2], in0=tiles[("part", q)][:, 0 : c2 - c1], in1=bias_s[:, N - (c2 - c1) : N], op=ALU.add
            )

        def finish_rest(q):
            c0, c1, c2 = split_column(q)
            nc.vector.scalar_tensor_tensor(
                out=o_all[:, c0:c1], in0=tiles[("h", PAIR * q + 1, BANKS - 1)][:, 0 : c1 - c0],
                scalar=tiles[("va", q)][:, 5, 1:2], in1=bias_s[:, BANK : BANK + c1 - c0], op0=ALU.mult, op1=ALU.add,
            )

        def time_column(q, i0=0, i1=PAIR):
            c0 = OUT_W * PAIR * q
            for i in range(i0, i1):
                nc.scalar.copy(
                    out=o_all[:, c0 + i * OUT_W : c0 + i * OUT_W + 1], in_=tiles[("roots", q + BEHIND)][:, 0, i : i + 1]
                )

        def store(c0, c1):
            cols = slice(c0 // ALIGN * ALIGN, c1 // ALIGN * ALIGN)
            nc.sync.dma_start(out=out_flat[:, cols], in_=o_all[:, cols])

        def last_pair(q):
            c0 = OUT_W * PAIR * q
            a, b = c0 + ALIGN, c0 + OUT_W + ALIGN
            dot_with_bias(q, 0, 0)
            dot_with_bias(q, 0, 1)
            dot_with_bias(q, 1, 0)
            row_factors(q, 0, 0, 1)
            row_factors(q, 1, 0, 1)
            dot_with_bias(q, 1, 1)
            row_factors(q, 2, 0, 1)
            row_factors(q, 0, 1, 2)
            row_factors(q, 3, 0, 1)
            row_factors(q, 1, 1, 2)
            time_square(q, 0, 0, 1)
            finish(q, 0, 0)
            time_square(q, 1, 0, 1)
            time_square(q, 2, 0, 1)
            time_root(q, 0)
            time_column(q, 0, 1)
            row_factors(q, 2, 1, 2)
            finish(q, 0, 1)
            store(a, c0 + OUT_W)
            row_factors(q, 3, 1, 2)
            time_square(q, 0, 1, 2)
            finish(q, 1, 0)
            store(b, c0 + OUT_W + 1 + BANK)
            time_square(q, 1, 1, 2)
            time_square(q, 2, 1, 2)
            time_root(q, 1)
            time_column(q, 1, 2)
            finish(q, 1, 1)
            store(c0 + OUT_W + 1 + BANK, c0 + PAIR * OUT_W)
            store(c0, a)
            store(c0 + OUT_W, b)

        def period(q):
            last = q + 1 == PAIRS - 1
            c0 = OUT_W * PAIR * q
            norm_of_h(q + 1, 0, 0)
            norm_of_h(q + 1, 0, 1)
            if last:
                roots_of_h(q + 1, 0, 1)
            scaled_part(q)
            finish_part(q)
            norm_of_h(q + 1, 1, 0)
            finish(q, 0, 0)
            multiply(PAIR * (q + 1) + 1, 1)
            time_square(q, 0)
            finish(q, 0, 1)
            time_square(q, 1)
            time_square(q, 2)
            roots(q + BEHIND)
            if last:
                exponentials(q + 1, 0, 1)
            if live(q + 2):
                regroup(PAIR * (q + 2))
            norm_of_h(q + 1, 1, 1)
            if last:
                roots_of_h(q + 1, 1, 2)
            else:
                roots_of_h(q + 1)
            if live(q + 2):
                turn(PAIR * (q + 2) + 1, clock=True)
            finish(q, 1, 0)
            finish_rest(q)
            if live(q + 4):
                norm_of_sp(q + 4, 0)
            time_column(q)
            store(c0, c0 + PAIR * OUT_W)
            if live(q + 2):
                regroup(PAIR * (q + 2) + 1)
            if last:
                exponentials(q + 1, 1, 2)
                last_pair(q + 1)
                return
            exponentials(q + 1)
            for i in range(PAIR):
                for nh in range(BANKS):
                    dot_with_bias(q + 1, i, nh)
            if live(q + 4):
                norm_of_sp(q + 4, 1)
            if live(q + 2):
                quantise(PAIR * (q + 2))
                multiply(PAIR * (q + 2), 0, clock=True)
                multiply(PAIR * (q + 2), 1)
            row_factors(q + 1, 0)
            if live(q + 3):
                row_scale(q + 3)
            row_factors(q + 1, 1)
            if live(q + 2):
                quantise(PAIR * (q + 2) + 1)
                multiply(PAIR * (q + 2) + 1, 0)
            row_factors(q + 1, 2)
            if live(q + 3):
                log_map(q + 3, 0)
                turn(PAIR * (q + 3))
            row_factors(q + 1, 3)
            if live(q + 3):
                log_map(q + 3, 1)

        V, S = nc.vector, nc.scalar
        bias_spread()
        norm_of_sp(0, 0)
        bias_copy(0)
        bias_square(1)
        bias_square(0)
        arccosh_square(x_head[:, :, 0], 0, TILES)
        arccosh_root(0, TILES)
        load_table(ACT.Ln)
        norm_of_sp(0, 1, on_vector=True)
        arccosh_sum(0, TILES)
        arccosh_log(0, TILES)
        load_table(ACT.Exp)
        roots(0)
        bias_root()
        bias_copy(1)
        weight_turn(0, 0, clock=True)
        weight_turn(0, 1)
        weight_turn(1, 0, clock=True)
        weight_turn(1, 1)
        weight_regroup(0, 0, V)
        row_scale(0)
        weight_regroup(0, 1, V)
        weight_turn(2, 0, clock=True)
        log_map(0, 0)
        turn(0)
        log_map(0, 1)
        weight_turn(2, 1)
        weight_regroup(1, 0, V)
        regroup(0)
        weight_turn(3, 0, clock=True)
        turn(1)
        weight_turn(3, 1)
        weight_regroup(1, 1, V)
        weight_quantise(0, 0)
        weight_quantise(0, 1)
        weight_quantise(1, 0)
        weight_quantise(1, 1)
        quantise(0)
        multiply(0, 0)
        bias_exps()
        weight_regroup(2, 0, S)
        regroup(1)
        bias_factors()
        weight_regroup(2, 1, V)
        quantise(1)
        multiply(1, 0)
        norm_of_sp(1, 0)
        norm_of_h(0, 0, 0)
        weight_quantise(2, 0)
        weight_regroup(3, 0, V)
        weight_quantise(2, 1)
        dot_with_bias(0, 0, 0)
        norm_of_sp(1, 1)
        roots(1)
        norm_of_h(0, 1, 0)
        weight_regroup(3, 1, V)
        weight_quantise(3, 0)
        weight_quantise(3, 1)
        multiply(0, 1, clock=True)
        multiply(1, 1)
        row_scale(1)
        dot_with_bias(0, 1, 0)
        log_map(1, 0)
        turn(2, clock=True)
        log_map(1, 1)
        norm_of_sp(2, 0)
        norm_of_h(0, 0, 1)
        norm_of_h(0, 1, 1)
        roots_of_h(0)
        regroup(2)
        turn(3)
        norm_of_sp(2, 1)
        roots(2)
        bias_scaled()
        dot_with_bias(0, 0, 1)
        dot_with_bias(0, 1, 1)
        quantise(2)
        multiply(2, 0)
        multiply(2, 1)
        exponentials(0)
        regroup(3)
        row_factors(0, 0)
        row_factors(0, 1)
        quantise(3)
        multiply(3, 0)
        row_factors(0, 2)
        row_scale(2)
        row_factors(0, 3)
        log_map(2, 0)
        turn(4)
        log_map(2, 1)
        norm_of_sp(3, 0)
        norm_of_sp(3, 1)
        for q in range(PAIRS - 1):
            period(q)
